import numpy as np
import ml_dtypes


def mxq(x, axis, fmt="e4m3"):
    dtype, down = {"e4m3": (ml_dtypes.float8_e4m3fn, 7), "e5m2": (ml_dtypes.float8_e5m2, 14)}[fmt]
    v = np.moveaxis(np.asarray(x, np.float32).astype(ml_dtypes.bfloat16).astype(np.float64), axis, -1)
    blocks = v.reshape(v.shape[:-1] + (-1, 32))
    amax = np.abs(blocks).max(-1, keepdims=True)
    byte = np.maximum(np.where(amax > 0, np.frexp(amax)[1] - 1 + 127, 0) - down, 1)
    scale = np.exp2(byte - 127.0)
    codes = (blocks / scale).astype(np.float32).astype(dtype).astype(np.float64)
    return np.moveaxis((codes * scale).reshape(v.shape), -1, axis)


WIDE = False


def mx_kscale(k):
    if not WIDE:
        return np.ones(k)
    levels = np.array([20, -20, 10, -10, 0])
    a = np.random.permutation(np.resize(levels, k // 512 * 4)).reshape(k // 512, 4)
    idx = np.arange(k)
    return np.exp2(a[idx // 512, idx % 128 // 32])


BF16 = ml_dtypes.bfloat16


def bf(x):
    return np.asarray(x, np.float32).astype(BF16)


def f64(x):
    return np.asarray(x).astype(np.float64)


N, CI, CO, H, W, KH, KW = 4, 512, 1024, 18, 18, 3, 3
HO, WO = H - KH + 1, W - KW + 1
L = N * HO * WO


def setup_inputs():
    s = mx_kscale(CO)
    x = np.random.standard_normal((N, CI, H, W))
    y = np.random.standard_normal((N, CO, HO, WO)) / np.sqrt(L) / s[None, :, None, None]
    g = np.random.standard_normal((CO, CI, KH, KW)) * np.exp2(np.random.randint(-12, 1, (1, CI, 1, 1))) * s[:, None, None, None]
    return {"input": bf(x), "grad_output": bf(y), "grad_out": bf(g)}


def reference(input, grad_output, grad_out):
    yq = mxq(f64(grad_output).transpose(1, 0, 2, 3).reshape(CO, L), 0, "e4m3")
    gq = mxq(f64(grad_out).reshape(CO, CI * KH * KW), 0, "e5m2").reshape(CO, CI, KH, KW)
    gx = np.zeros((N, CI, H, W))
    for i in range(KH):
        for j in range(KW):
            t = gq[:, :, i, j].T @ yq
            gx[:, :, i:i + HO, j:j + WO] += t.reshape(CI, N, HO, WO).transpose(1, 0, 2, 3)
    return gx

@@ -1,0 +1,266 @@
+import concourse.mybir as mybir
+from concourse.masks import make_identity
+
+F32 = mybir.dt.float32
+BF16 = mybir.dt.bfloat16
+I32 = mybir.dt.int32
+U32 = mybir.dt.uint32
+U8 = mybir.dt.uint8
+E4M3_X4 = mybir.dt.float8_e4m3fn_x4
+E5M2_X4 = mybir.dt.float8_e5m2_x4
+
+P = 128
+PACK = 4
+K_PASS = P * PACK
+
+IMAGES = 4
+CI = 512
+CO = 1024
+HO = 16
+WO = 16
+H = 18
+W = 18
+KH = 3
+KW = 3
+TAPS = KH * KW
+PASSES = CO // K_PASS
+C_TILES = CI // P
+BANK = 512
+
+GROUP = WO * IMAGES
+Y_GROUPS = HO + 2
+Y_COLS = Y_GROUPS * GROUP
+ROWS_PER_BANK = BANK // GROUP
+CORE_BANKS = HO // ROWS_PER_BANK
+G_COLS = P * TAPS
+
+VECTOR_TAPS = 5
+Y_VECTOR_ROWS = 10
+
+FLOPS = 2 * TAPS * CO * CI * IMAGES * HO * WO
+BYTES = 2 * IMAGES * CO * HO * WO + 2 * CO * CI * TAPS + 4 * IMAGES * CI * H * W
+
+
+def tile_model_pa_kernel(tc, image_in, grad_output, grad_out, out):
+    nc = tc.nc
+    with tc.tile_pool(name="keep", bufs=1) as keep, tc.tile_pool(name="g_in", bufs=4) as g_in, tc.tile_pool(
+        name="g_mid", bufs=3
+    ) as g_mid, tc.psum_pool(name="core_psum", bufs=2) as core_psum, tc.psum_pool(
+        name="edge_psum", bufs=1
+    ) as edge_psum:
+        y_codes = keep.tile([P, PASSES, KW, Y_COLS], U32, align_bytes=64)
+        y_scales = keep.tile([P, PASSES, KW, Y_COLS], U8, align_bytes=64)
+        g_codes = keep.tile([P, PASSES, TAPS, CI], U32, align_bytes=64)
+        g_scales = keep.tile([P, PASSES, TAPS, CI], U8, align_bytes=64)
+        col_codes = keep.tile([P, PASSES, 2, KH, P], U32, align_bytes=64)
+        col_scales = keep.tile([P, PASSES, 2, KH, P], U8, align_bytes=64)
+        image = keep.tile([P, C_TILES, IMAGES, H, W], F32)
+        identity = keep.tile([P, P], F32)
+
+        y_codes_i = y_codes[:].bitcast(I32)
+        y_scales_i = y_scales[:].bitcast(I32)
+        col_codes_i = col_codes[:].bitcast(I32)
+        col_scales_i = col_scales[:].bitcast(I32)
+
+        nc.vector.memset(y_codes_i, 0)
+        nc.vector.memset(y_scales_i, 0)
+        nc.gpsimd.memset(col_codes[:].bitcast(F32), 0.0)
+        nc.gpsimd.memset(col_scales[:].bitcast(F32), 0.0)
+        make_identity(nc, identity[:])
+
+        def load_y(kp):
+            y_raw = keep.tile([P, IMAGES * PACK, HO * WO], BF16, name="y_raw%d" % kp)
+            nc.sync.dma_start(
+                out=y_raw[:].rearrange("p (n t) x -> p n (t x)", t=PACK),
+                in_=grad_output[:, kp * K_PASS : (kp + 1) * K_PASS].rearrange("n (p t) i j -> p n (t i j)", t=PACK),
+            )
+            return y_raw
+
+        def load_g(kp, ct):
+            g_raw = g_in.tile([P, PACK, G_COLS], BF16, name="g_raw")
+            nc.sync.dma_start(
+                out=g_raw[:],
+                in_=grad_out[kp * K_PASS : (kp + 1) * K_PASS, ct * P : (ct + 1) * P].rearrange(
+                    "(p t) c kh kw -> p t (c kh kw)", t=PACK
+                ),
+            )
+            return g_raw
+
+        def prepare_y(kp, y_raw):
+            y_grouped = keep.tile([P, HO * WO, IMAGES * PACK], BF16, align_bytes=64, name="y_grouped%d" % kp)
+            split = Y_VECTOR_ROWS * WO
+            turned = y_raw[:].rearrange("p m x -> p x m")
+            nc.vector.tensor_copy(out=y_grouped[:, :split], in_=turned[:, :split])
+            nc.scalar.copy(out=y_grouped[:, split:], in_=turned[:, split:])
+            inner = slice(GROUP, GROUP + HO * GROUP)
+            nc.vector.quantize_mx(
+                out=y_codes[:, kp, 1, inner].bitcast(E4M3_X4),
+                scales=y_scales[:, kp, 1, inner],
+                in_=y_grouped[:].rearrange("p x m -> p (x m)"),
+            )
+            for view, slot in ((y_codes_i, IMAGES), (y_scales_i, 1)):
+                width = WO * slot
+                rows = slice(width, width + HO * width)
+                middle = view[:, kp, 1, rows].rearrange("p (i c) -> p i c", c=width)
+                left = view[:, kp, 0, rows].rearrange("p (i c) -> p i c", c=width)
+                right = view[:, kp, 2, rows].rearrange("p (i c) -> p i c", c=width)
+                nc.vector.tensor_copy(out=left[:, :, : width - slot], in_=middle[:, :, slot:])
+                nc.vector.tensor_copy(out=right[:, :, slot:], in_=middle[:, :, : width - slot])
+
+        def prepare_columns():
+            for view, cols, slot in ((y_codes_i, col_codes_i, IMAGES), (y_scales_i, col_scales_i, 1)):
+                width = WO * slot
+                rows = slice(width, width + HO * width)
+                middle = view[:, :, 1, rows].rearrange("p k (i u s) -> p k i u s", u=WO, s=slot)
+                for side, u in enumerate((0, WO - 1)):
+                    for kh in range(KH):
+                        nc.vector.tensor_copy(
+                            out=cols[:, :, side, kh, kh * slot : (kh + HO) * slot].rearrange(
+                                "p k (i s) -> p k i s", s=slot
+                            ),
+                            in_=middle[:, :, :, u, :],
+                        )
+
+        def regroup_g(g_raw):
+            g_grouped = g_mid.tile([P, TAPS, P, PACK], BF16, align_bytes=64, name="g_grouped")
+            turned = g_raw[:].rearrange("p t (c x) -> p x c t", x=TAPS)
+            nc.vector.tensor_copy(out=g_grouped[:, :VECTOR_TAPS], in_=turned[:, :VECTOR_TAPS])
+            nc.scalar.copy(out=g_grouped[:, VECTOR_TAPS:], in_=turned[:, VECTOR_TAPS:])
+            return g_grouped
+
+        def quantise_g(kp, ct, g_grouped):
+            for tap in range(TAPS):
+                nc.vector.quantize_mx(
+                    out=g_codes[:, kp, tap, ct * P : (ct + 1) * P].bitcast(E5M2_X4),
+                    scales=g_scales[:, kp, tap, ct * P : (ct + 1) * P],
+                    in_=g_grouped[:, tap].rearrange("p c t -> p (c t)"),
+                )
+
+        def core_passes(ct, kp, banks):
+            for kh in range(KH):
+                for kw in range(KW):
+                    tap = kh * KW + kw
+                    for b in range(CORE_BANKS):
+                        first = (b * ROWS_PER_BANK + 2 - kh) * GROUP
+                        nc.tensor.matmul_mx(
+                            out=banks[b][:],
+                            lhsT=g_codes[:, kp, tap, ct * P : (ct + 1) * P].bitcast(E5M2_X4),
+                            lhsT_scale=g_scales[:, kp, tap, ct * P : (ct + 1) * P],
+                            rhs=y_codes[:, kp, kw, first : first + BANK].bitcast(E4M3_X4),
+                            rhs_scale=y_scales[:, kp, kw, first : first + BANK],
+                            start=(kp == 0 and tap == 0),
+                            stop=(kp == PASSES - 1 and tap == TAPS - 1),
+                        )
+
+        def core_banks():
+            return [core_psum.tile([P, BANK], F32, name="core%d" % b) for b in range(CORE_BANKS)]
+
+        def core_out(ct, banks):
+            for b in range(CORE_BANKS):
+                top = 1 + b * ROWS_PER_BANK
+                nc.scalar.copy(
+                    out=image[:, ct, :, top : top + ROWS_PER_BANK, 1 : 1 + WO],
+                    in_=banks[b][:].rearrange("c (r u n) -> c n r u", u=WO, n=IMAGES),
+                )
+
+        def edge_pass(bank, codes, scales, kp, tap, start, stop):
+            nc.tensor.matmul_mx(
+                out=bank[:],
+                lhsT=codes.bitcast(E4M3_X4),
+                lhsT_scale=scales,
+                rhs=g_codes[:, kp, tap, :].bitcast(E5M2_X4),
+                rhs_scale=g_scales[:, kp, tap, :],
+                start=start,
+                stop=stop,
+            )
+
+        def store(ct):
+            nc.sync.dma_start(
+                out=out[:, ct * P : (ct + 1) * P].rearrange("n c h w -> c n (h w)"),
+                in_=image[:, ct].rearrange("c n h w -> c n (h w)"),
+            )
+
+        chunks = [(kp, ct) for ct in range(C_TILES) for kp in range(PASSES)]
+        y_raws = []
+        g_raws = []
+        for kp in range(PASSES):
+            y_raws.append(load_y(kp))
+            g_raws.append(load_g(*chunks[kp]))
+        for kp in range(PASSES):
+            prepare_y(kp, y_raws[kp])
+        waiting = None
+        for index, (kp, ct) in enumerate(chunks):
+            g_raw = g_raws[index] if index < PASSES else load_g(kp, ct)
+            g_grouped = regroup_g(g_raw)
+            if waiting is not None:
+                quantise_g(*waiting)
+            waiting = (kp, ct, g_grouped)
+        quantise_g(*waiting)
+        prepare_columns()
+
+        for ct in range(C_TILES - 1):
+            banks = core_banks()
+            for kp in range(PASSES):
+                core_passes(ct, kp, banks)
+            core_out(ct, banks)
+
+        rows_bank = edge_psum.tile([P, BANK], F32, name="rows_bank", tag="edge0")
+        left_bank = edge_psum.tile([P, BANK], F32, name="left_bank", tag="edge1")
+        right_bank = edge_psum.tile([P, BANK], F32, name="right_bank", tag="edge2")
+        for kp in range(PASSES):
+            for kh, first in ((KH - 1, HO * GROUP), (0, 0)):
+                for kw in range(KW):
+                    edge_pass(
+                        rows_bank,
+                        y_codes[:, kp, kw, first : first + P],
+                        y_scales[:, kp, kw, first : first + P],
+                        kp,
+                        kh * KW + kw,
+                        start=(kp == 0 and kh == KH - 1 and kw == 0),
+                        stop=(kp == PASSES - 1 and kh == 0 and kw == KW - 1),
+                    )
+        for side, (bank, kw) in enumerate(((left_bank, 0), (right_bank, KW - 1))):
+            for kp in range(PASSES):
+                for kh in range(KH):
+                    edge_pass(
+                        bank,
+                        col_codes[:, kp, side, kh, :],
+                        col_scales[:, kp, side, kh, :],
+                        kp,
+                        kh * KW + kw,
+                        start=(kp == 0 and kh == 0),
+                        stop=(kp == PASSES - 1 and kh == KH - 1),
+                    )
+        edges = []
+        for e, bank in enumerate((rows_bank, left_bank, right_bank)):
+            edge = keep.tile([P, CI], F32, name="edge%d" % e)
+            nc.vector.tensor_copy(out=edge[:], in_=bank[:])
+            edges.append(edge)
+
+        last = C_TILES - 1
+        banks = core_banks()
+        core_passes(last, 0, banks)
+
+        flipped = []
+        for e, edge in enumerate(edges):
+            flip = edge_psum.tile([P, C_TILES, P], F32, name="flip%d" % e, tag="edge%d" % e)
+            for ct in range(C_TILES):
+                nc.tensor.transpose(flip[:, ct, :], edge[:, ct * P : (ct + 1) * P], identity[:])
+            flipped.append(flip)
+        rows_flip, left_flip, right_flip = flipped
+        for half, p in enumerate((H - 1, 0)):
+            nc.scalar.copy(
+                out=image[:, :, :, p, 1 : 1 + WO],
+                in_=rows_flip[:, :, half * GROUP : (half + 1) * GROUP].rearrange("c t (u n) -> c t n u", n=IMAGES),
+            )
+        for flip, q in ((left_flip, 0), (right_flip, W - 1)):
+            nc.scalar.copy(
+                out=image[:, :, :, :, q],
+                in_=flip[:, :, : H * IMAGES].rearrange("c t (p n) -> c t n p", n=IMAGES),
+            )
+        for ct in range(last):
+            store(ct)
+
+        core_passes(last, 1, banks)
+        core_out(last, banks)
+        store(last)

@@ -34,8 +34,9 @@ ROWS_PER_BANK = BANK // GROUP
 CORE_BANKS = HO // ROWS_PER_BANK
 G_COLS = P * TAPS
 
-VECTOR_TAPS = 5
+VECTOR_KH = 2
 Y_VECTOR_ROWS = 10
+G_BUFS = 4
 
 FLOPS = 2 * TAPS * CO * CI * IMAGES * HO * WO
 BYTES = 2 * IMAGES * CO * HO * WO + 2 * CO * CI * TAPS + 4 * IMAGES * CI * H * W
@@ -43,11 +44,9 @@ BYTES = 2 * IMAGES * CO * HO * WO + 2 * CO * CI * TAPS + 4 * IMAGES * CI * H * W
 
 def tile_model_pa_kernel(tc, image_in, grad_output, grad_out, out):
     nc = tc.nc
-    with tc.tile_pool(name="keep", bufs=1) as keep, tc.tile_pool(name="g_in", bufs=4) as g_in, tc.tile_pool(
+    with tc.tile_pool(name="keep", bufs=1) as keep, tc.tile_pool(name="g_in", bufs=G_BUFS) as g_in, tc.tile_pool(
         name="g_mid", bufs=3
-    ) as g_mid, tc.psum_pool(name="core_psum", bufs=2) as core_psum, tc.psum_pool(
-        name="edge_psum", bufs=1
-    ) as edge_psum:
+    ) as g_mid, tc.psum_pool(name="psum", bufs=1) as psum, tc.manual_schedule():
         y_codes = keep.tile([P, PASSES, KW, Y_COLS], U32, align_bytes=64)
         y_scales = keep.tile([P, PASSES, KW, Y_COLS], U8, align_bytes=64)
         g_codes = keep.tile([P, PASSES, TAPS, CI], U32, align_bytes=64)
@@ -57,21 +56,28 @@ def tile_model_pa_kernel(tc, image_in, grad_output, grad_out, out):
         image = keep.tile([P, C_TILES, IMAGES, H, W], F32)
         identity = keep.tile([P, P], F32)
 
-        y_codes_i = y_codes[:].bitcast(I32)
-        y_scales_i = y_scales[:].bitcast(I32)
-        col_codes_i = col_codes[:].bitcast(I32)
-        col_scales_i = col_scales[:].bitcast(I32)
+        y_views = ((y_codes[:].bitcast(I32), IMAGES), (y_scales[:].bitcast(I32), 1))
+        col_views = (col_codes[:].bitcast(I32), col_scales[:].bitcast(I32))
 
-        nc.vector.memset(y_codes_i, 0)
-        nc.vector.memset(y_scales_i, 0)
+        def y_rows(view, slot, kp, kw):
+            width = WO * slot
+            return view[:, kp, kw, width : (HO + 1) * width].rearrange("p (i c) -> p i c", c=width)
+
+        for view, slot in y_views:
+            width = WO * slot
+            nc.vector.memset(view[:, :, :, :width], 0)
+            nc.vector.memset(view[:, :, :, (HO + 1) * width :], 0)
+            for kp in range(PASSES):
+                nc.vector.memset(y_rows(view, slot, kp, 0)[:, :, width - slot :], 0)
+                nc.vector.memset(y_rows(view, slot, kp, 2)[:, :, :slot], 0)
         nc.gpsimd.memset(col_codes[:].bitcast(F32), 0.0)
         nc.gpsimd.memset(col_scales[:].bitcast(F32), 0.0)
         make_identity(nc, identity[:])
 
         def load_y(kp):
-            y_raw = keep.tile([P, IMAGES * PACK, HO * WO], BF16, name="y_raw%d" % kp)
+            y_raw = keep.tile([P, IMAGES, PACK, HO * WO], BF16, name="y_raw%d" % kp)
             nc.sync.dma_start(
-                out=y_raw[:].rearrange("p (n t) x -> p n (t x)", t=PACK),
+                out=y_raw[:].rearrange("p n t x -> p n (t x)"),
                 in_=grad_output[:, kp * K_PASS : (kp + 1) * K_PASS].rearrange("n (p t) i j -> p n (t i j)", t=PACK),
             )
             return y_raw
@@ -86,32 +92,35 @@ def tile_model_pa_kernel(tc, image_in, grad_output, grad_out, out):
             )
             return g_raw
 
-        def prepare_y(kp, y_raw):
-            y_grouped = keep.tile([P, HO * WO, IMAGES * PACK], BF16, align_bytes=64, name="y_grouped%d" % kp)
+        def regroup_y(kp, y_raw):
+            y_grouped = keep.tile([P, HO * WO, IMAGES, PACK], BF16, align_bytes=64, name="y_grouped%d" % kp)
             split = Y_VECTOR_ROWS * WO
-            turned = y_raw[:].rearrange("p m x -> p x m")
-            nc.vector.tensor_copy(out=y_grouped[:, :split], in_=turned[:, :split])
-            nc.scalar.copy(out=y_grouped[:, split:], in_=turned[:, split:])
-            inner = slice(GROUP, GROUP + HO * GROUP)
+            nc.vector.tensor_copy(
+                out=y_grouped[:, :split].rearrange("p x n t -> p n x t"),
+                in_=y_raw[:, :, :, :split].rearrange("p n t x -> p n x t"),
+            )
+            nc.scalar.copy(
+                out=y_grouped[:, split:].rearrange("p x n t -> p n x t"),
+                in_=y_raw[:, :, :, split:].rearrange("p n t x -> p n x t"),
+            )
+            return y_grouped
+
+        def quantise_y(kp, y_grouped):
+            inner = slice(GROUP, (HO + 1) * GROUP)
             nc.vector.quantize_mx(
                 out=y_codes[:, kp, 1, inner].bitcast(E4M3_X4),
                 scales=y_scales[:, kp, 1, inner],
-                in_=y_grouped[:].rearrange("p x m -> p (x m)"),
+                in_=y_grouped[:].rearrange("p x n t -> p (x n t)"),
             )
-            for view, slot in ((y_codes_i, IMAGES), (y_scales_i, 1)):
-                width = WO * slot
-                rows = slice(width, width + HO * width)
-                middle = view[:, kp, 1, rows].rearrange("p (i c) -> p i c", c=width)
-                left = view[:, kp, 0, rows].rearrange("p (i c) -> p i c", c=width)
-                right = view[:, kp, 2, rows].rearrange("p (i c) -> p i c", c=width)
-                nc.vector.tensor_copy(out=left[:, :, : width - slot], in_=middle[:, :, slot:])
-                nc.vector.tensor_copy(out=right[:, :, slot:], in_=middle[:, :, : width - slot])
+            for view, slot in y_views:
+                middle = y_rows(view, slot, kp, 1)
+                nc.vector.tensor_copy(out=y_rows(view, slot, kp, 0)[:, :, : (WO - 1) * slot], in_=middle[:, :, slot:])
+                nc.vector.tensor_copy(out=y_rows(view, slot, kp, 2)[:, :, slot:], in_=middle[:, :, : (WO - 1) * slot])
 
         def prepare_columns():
-            for view, cols, slot in ((y_codes_i, col_codes_i, IMAGES), (y_scales_i, col_scales_i, 1)):
+            for (view, slot), cols in zip(y_views, col_views):
                 width = WO * slot
-                rows = slice(width, width + HO * width)
-                middle = view[:, :, 1, rows].rearrange("p k (i u s) -> p k i u s", u=WO, s=slot)
+                middle = view[:, :, 1, width : (HO + 1) * width].rearrange("p k (i u s) -> p k i u s", u=WO, s=slot)
                 for side, u in enumerate((0, WO - 1)):
                     for kh in range(KH):
                         nc.vector.tensor_copy(
@@ -123,9 +132,11 @@ def tile_model_pa_kernel(tc, image_in, grad_output, grad_out, out):
 
         def regroup_g(g_raw):
             g_grouped = g_mid.tile([P, TAPS, P, PACK], BF16, align_bytes=64, name="g_grouped")
-            turned = g_raw[:].rearrange("p t (c x) -> p x c t", x=TAPS)
-            nc.vector.tensor_copy(out=g_grouped[:, :VECTOR_TAPS], in_=turned[:, :VECTOR_TAPS])
-            nc.scalar.copy(out=g_grouped[:, VECTOR_TAPS:], in_=turned[:, VECTOR_TAPS:])
+            turned = g_raw[:].rearrange("p t (c x) -> p c x t", x=TAPS)
+            for kh in range(KH):
+                taps = slice(kh * KW, (kh + 1) * KW)
+                copy = nc.vector.tensor_copy if kh < VECTOR_KH else nc.scalar.copy
+                copy(out=g_grouped[:, taps].rearrange("p x c t -> p c x t"), in_=turned[:, :, taps])
             return g_grouped
 
         def quantise_g(kp, ct, g_grouped):
@@ -136,24 +147,20 @@ def tile_model_pa_kernel(tc, image_in, grad_output, grad_out, out):
                     in_=g_grouped[:, tap].rearrange("p c t -> p (c t)"),
                 )
 
-        def core_passes(ct, kp, banks):
-            for kh in range(KH):
-                for kw in range(KW):
-                    tap = kh * KW + kw
-                    for b in range(CORE_BANKS):
-                        first = (b * ROWS_PER_BANK + 2 - kh) * GROUP
-                        nc.tensor.matmul_mx(
-                            out=banks[b][:],
-                            lhsT=g_codes[:, kp, tap, ct * P : (ct + 1) * P].bitcast(E5M2_X4),
-                            lhsT_scale=g_scales[:, kp, tap, ct * P : (ct + 1) * P],
-                            rhs=y_codes[:, kp, kw, first : first + BANK].bitcast(E4M3_X4),
-                            rhs_scale=y_scales[:, kp, kw, first : first + BANK],
-                            start=(kp == 0 and tap == 0),
-                            stop=(kp == PASSES - 1 and tap == TAPS - 1),
-                        )
-
-        def core_banks():
-            return [core_psum.tile([P, BANK], F32, name="core%d" % b) for b in range(CORE_BANKS)]
+        def core_passes(ct, kp, kh, banks):
+            for kw in range(KW):
+                tap = kh * KW + kw
+                for b in range(CORE_BANKS):
+                    first = (b * ROWS_PER_BANK + 2 - kh) * GROUP
+                    nc.tensor.matmul_mx(
+                        out=banks[b][:],
+                        lhsT=g_codes[:, kp, tap, ct * P : (ct + 1) * P].bitcast(E5M2_X4),
+                        lhsT_scale=g_scales[:, kp, tap, ct * P : (ct + 1) * P],
+                        rhs=y_codes[:, kp, kw, first : first + BANK].bitcast(E4M3_X4),
+                        rhs_scale=y_scales[:, kp, kw, first : first + BANK],
+                        start=(kp == 0 and tap == 0),
+                        stop=(kp == PASSES - 1 and tap == TAPS - 1),
+                    )
 
         def core_out(ct, banks):
             for b in range(CORE_BANKS):
@@ -180,33 +187,55 @@ def tile_model_pa_kernel(tc, image_in, grad_output, grad_out, out):
                 in_=image[:, ct].rearrange("c n h w -> c n (h w)"),
             )
 
-        chunks = [(kp, ct) for ct in range(C_TILES) for kp in range(PASSES)]
-        y_raws = []
-        g_raws = []
+        chunks = [(kp, pair + ct) for pair in range(0, C_TILES, 2) for kp in range(PASSES) for ct in range(2)]
+        raws = {}
         for kp in range(PASSES):
-            y_raws.append(load_y(kp))
-            g_raws.append(load_g(*chunks[kp]))
-        for kp in range(PASSES):
-            prepare_y(kp, y_raws[kp])
-        waiting = None
-        for index, (kp, ct) in enumerate(chunks):
-            g_raw = g_raws[index] if index < PASSES else load_g(kp, ct)
-            g_grouped = regroup_g(g_raw)
-            if waiting is not None:
-                quantise_g(*waiting)
-            waiting = (kp, ct, g_grouped)
-        quantise_g(*waiting)
+            raws["y", kp] = load_y(kp)
+            for ct in range(2):
+                raws[kp, ct] = load_g(kp, ct)
+
+        def regroup(kp, ct):
+            y_grouped = regroup_y(kp, raws["y", kp]) if ct == 0 else None
+            return y_grouped, regroup_g(raws[kp, ct])
+
+        def quantise(kp, ct, grouped):
+            y_grouped, g_grouped = grouped
+            if ct == 0:
+                quantise_y(kp, y_grouped)
+            quantise_g(kp, ct, g_grouped)
+
+        banks = {}
+
+        def core(kp, ct):
+            if kp == 0:
+                banks[ct] = [psum.tile([P, BANK], F32, name="core%d%d" % (ct % 2, b)) for b in range(CORE_BANKS)]
+            for kh in range(KH):
+                core_passes(ct, kp, kh, banks[ct])
+
+        quantise_y(0, regroup_y(0, raws["y", 0]))
+        quantise_g(0, 0, regroup_g(raws[0, 0]))
+        core(0, 0)
+        grouped = regroup(*chunks[1])
+        full = None
+        for index in range(1, len(chunks)):
+            kp, ct = chunks[index]
+            if index + G_BUFS - 1 < len(chunks):
+                raws[chunks[index + G_BUFS - 1]] = load_g(*chunks[index + G_BUFS - 1])
+            following = regroup(*chunks[index + 1]) if index + 1 < len(chunks) else None
+            if full is not None:
+                core_out(full, banks[full])
+                full = None
+            quantise(kp, ct, grouped)
+            grouped = following
+            if index + 1 < len(chunks):
+                core(kp, ct)
+                if kp == PASSES - 1:
+                    full = ct
         prepare_columns()
 
-        for ct in range(C_TILES - 1):
-            banks = core_banks()
-            for kp in range(PASSES):
-                core_passes(ct, kp, banks)
-            core_out(ct, banks)
-
-        rows_bank = edge_psum.tile([P, BANK], F32, name="rows_bank", tag="edge0")
-        left_bank = edge_psum.tile([P, BANK], F32, name="left_bank", tag="edge1")
-        right_bank = edge_psum.tile([P, BANK], F32, name="right_bank", tag="edge2")
+        rows_bank = psum.tile([P, BANK], F32, name="rows_bank", tag="edge0")
+        left_bank = psum.tile([P, BANK], F32, name="left_bank", tag="edge1")
+        right_bank = psum.tile([P, BANK], F32, name="right_bank", tag="edge2")
         for kp in range(PASSES):
             for kh, first in ((KH - 1, HO * GROUP), (0, 0)):
                 for kw in range(KW):
@@ -237,16 +266,17 @@ def tile_model_pa_kernel(tc, image_in, grad_output, grad_out, out):
             nc.vector.tensor_copy(out=edge[:], in_=bank[:])
             edges.append(edge)
 
-        last = C_TILES - 1
-        banks = core_banks()
-        core_passes(last, 0, banks)
-
+        last_kp, last_ct = chunks[-1]
+        core_passes(last_ct, last_kp, 0, banks[last_ct])
         flipped = []
         for e, edge in enumerate(edges):
-            flip = edge_psum.tile([P, C_TILES, P], F32, name="flip%d" % e, tag="edge%d" % e)
+            flip = psum.tile([P, C_TILES, P], F32, name="flip%d" % e, tag="edge%d" % e)
             for ct in range(C_TILES):
                 nc.tensor.transpose(flip[:, ct, :], edge[:, ct * P : (ct + 1) * P], identity[:])
             flipped.append(flip)
+        for kh in range(1, KH):
+            core_passes(last_ct, last_kp, kh, banks[last_ct])
+
         rows_flip, left_flip, right_flip = flipped
         for half, p in enumerate((H - 1, 0)):
             nc.scalar.copy(
@@ -258,9 +288,8 @@ def tile_model_pa_kernel(tc, image_in, grad_output, grad_out, out):
                 out=image[:, :, :, :, q],
                 in_=flip[:, :, : H * IMAGES].rearrange("c t (p n) -> c t n p", n=IMAGES),
             )
-        for ct in range(last):
-            store(ct)
-
-        core_passes(last, 1, banks)
-        core_out(last, banks)
-        store(last)
+        for ct in range(C_TILES):
+            if ct != last_ct:
+                store(ct)
+        core_out(last_ct, banks[last_ct])
+        store(last_ct)

@@ -34,7 +34,7 @@ ROWS_PER_BANK = BANK // GROUP
 CORE_BANKS = HO // ROWS_PER_BANK
 G_COLS = P * TAPS
 
-VECTOR_KH = 2
+VECTOR_C = 64
 Y_VECTOR_ROWS = 10
 G_BUFS = 4
 
@@ -53,7 +53,14 @@ def tile_model_pa_kernel(tc, image_in, grad_output, grad_out, out):
         g_scales = keep.tile([P, PASSES, TAPS, CI], U8, align_bytes=64)
         col_codes = keep.tile([P, PASSES, 2, KH, P], U32, align_bytes=64)
         col_scales = keep.tile([P, PASSES, 2, KH, P], U8, align_bytes=64)
-        image = keep.tile([P, C_TILES, IMAGES, H, W], F32)
+        images = [keep.tile([P, IMAGES, H, W], F32, name="image%d" % ct) for ct in range(C_TILES)]
+
+        def copy_to_image(ct, dst, src):
+            if ct < C_TILES // 2:
+                nc.scalar.copy(out=dst, in_=src)
+            else:
+                nc.vector.tensor_copy(out=dst, in_=src)
+
         identity = keep.tile([P, P], F32)
 
         y_views = ((y_codes[:].bitcast(I32), IMAGES), (y_scales[:].bitcast(I32), 1))
@@ -135,8 +142,9 @@ def tile_model_pa_kernel(tc, image_in, grad_output, grad_out, out):
             turned = g_raw[:].rearrange("p t (c x) -> p c x t", x=TAPS)
             for kh in range(KH):
                 taps = slice(kh * KW, (kh + 1) * KW)
-                copy = nc.vector.tensor_copy if kh < VECTOR_KH else nc.scalar.copy
-                copy(out=g_grouped[:, taps].rearrange("p x c t -> p c x t"), in_=turned[:, :, taps])
+                regions = g_grouped[:, taps].rearrange("p x c t -> p c x t")
+                nc.vector.tensor_copy(out=regions[:, :VECTOR_C], in_=turned[:, :VECTOR_C, taps])
+                nc.scalar.copy(out=regions[:, VECTOR_C:], in_=turned[:, VECTOR_C:, taps])
             return g_grouped
 
         def quantise_g(kp, ct, g_grouped):
@@ -165,9 +173,10 @@ def tile_model_pa_kernel(tc, image_in, grad_output, grad_out, out):
         def core_out(ct, banks):
             for b in range(CORE_BANKS):
                 top = 1 + b * ROWS_PER_BANK
-                nc.scalar.copy(
-                    out=image[:, ct, :, top : top + ROWS_PER_BANK, 1 : 1 + WO],
-                    in_=banks[b][:].rearrange("c (r u n) -> c n r u", u=WO, n=IMAGES),
+                copy_to_image(
+                    ct,
+                    dst=images[ct][:, :, top : top + ROWS_PER_BANK, 1 : 1 + WO],
+                    src=banks[b][:].rearrange("c (r u n) -> c n r u", u=WO, n=IMAGES),
                 )
 
         def edge_pass(bank, codes, scales, kp, tap, start, stop):
@@ -184,7 +193,7 @@ def tile_model_pa_kernel(tc, image_in, grad_output, grad_out, out):
         def store(ct):
             nc.sync.dma_start(
                 out=out[:, ct * P : (ct + 1) * P].rearrange("n c h w -> c n (h w)"),
-                in_=image[:, ct].rearrange("c n h w -> c n (h w)"),
+                in_=images[ct][:].rearrange("c n h w -> c n (h w)"),
             )
 
         chunks = [(kp, pair + ct) for pair in range(0, C_TILES, 2) for kp in range(PASSES) for ct in range(2)]
@@ -217,21 +226,23 @@ def tile_model_pa_kernel(tc, image_in, grad_output, grad_out, out):
         core(0, 0)
         grouped = regroup(*chunks[1])
         full = None
-        for index in range(1, len(chunks)):
+        for index in range(1, len(chunks) - 1):
             kp, ct = chunks[index]
             if index + G_BUFS - 1 < len(chunks):
                 raws[chunks[index + G_BUFS - 1]] = load_g(*chunks[index + G_BUFS - 1])
-            following = regroup(*chunks[index + 1]) if index + 1 < len(chunks) else None
+            following = regroup(*chunks[index + 1])
             if full is not None:
                 core_out(full, banks[full])
                 full = None
             quantise(kp, ct, grouped)
             grouped = following
-            if index + 1 < len(chunks):
-                core(kp, ct)
-                if kp == PASSES - 1:
-                    full = ct
+            core(kp, ct)
+            if kp == PASSES - 1:
+                full = ct
+        last_kp, last_ct = chunks[-1]
+        quantise(last_kp, last_ct, grouped)
         prepare_columns()
+        core_out(full, banks[full])
 
         rows_bank = psum.tile([P, BANK], F32, name="rows_bank", tag="edge0")
         left_bank = psum.tile([P, BANK], F32, name="left_bank", tag="edge1")
@@ -266,30 +277,31 @@ def tile_model_pa_kernel(tc, image_in, grad_output, grad_out, out):
             nc.vector.tensor_copy(out=edge[:], in_=bank[:])
             edges.append(edge)
 
-        last_kp, last_ct = chunks[-1]
         core_passes(last_ct, last_kp, 0, banks[last_ct])
-        flipped = []
-        for e, edge in enumerate(edges):
-            flip = psum.tile([P, C_TILES, P], F32, name="flip%d" % e, tag="edge%d" % e)
-            for ct in range(C_TILES):
-                nc.tensor.transpose(flip[:, ct, :], edge[:, ct * P : (ct + 1) * P], identity[:])
-            flipped.append(flip)
+        flips = []
+        for ct in range(C_TILES):
+            flip = psum.tile([P, len(edges), P], F32, name="flip%d" % ct, tag="edge%d" % ct)
+            for e, edge in enumerate(edges):
+                nc.tensor.transpose(flip[:, e, :], edge[:, ct * P : (ct + 1) * P], identity[:])
+            flips.append(flip)
         for kh in range(1, KH):
             core_passes(last_ct, last_kp, kh, banks[last_ct])
 
-        rows_flip, left_flip, right_flip = flipped
-        for half, p in enumerate((H - 1, 0)):
-            nc.scalar.copy(
-                out=image[:, :, :, p, 1 : 1 + WO],
-                in_=rows_flip[:, :, half * GROUP : (half + 1) * GROUP].rearrange("c t (u n) -> c t n u", n=IMAGES),
+        def rim_out(ct):
+            for half, p in enumerate((H - 1, 0)):
+                copy_to_image(
+                    ct,
+                    dst=images[ct][:, :, p, 1 : 1 + WO],
+                    src=flips[ct][:, 0, half * GROUP : (half + 1) * GROUP].rearrange("c (u n) -> c n u", n=IMAGES),
+                )
+            copy_to_image(
+                ct,
+                dst=images[ct][:, :, :, 0 : W : W - 1],
+                src=flips[ct][:, 1:, : H * IMAGES].rearrange("c e (p n) -> c n p e", n=IMAGES),
             )
-        for flip, q in ((left_flip, 0), (right_flip, W - 1)):
-            nc.scalar.copy(
-                out=image[:, :, :, :, q],
-                in_=flip[:, :, : H * IMAGES].rearrange("c t (p n) -> c t n p", n=IMAGES),
-            )
-        for ct in range(C_TILES):
-            if ct != last_ct:
-                store(ct)
-        core_out(last_ct, banks[last_ct])
-        store(last_ct)
+
+        for ct in (0, 2, 1, 3):
+            rim_out(ct)
+            if ct == last_ct:
+                core_out(ct, banks[ct])
+            store(ct)

@@ -32,11 +32,14 @@ Y_GROUPS = HO + 2
 Y_COLS = Y_GROUPS * GROUP
 ROWS_PER_BANK = BANK // GROUP
 CORE_BANKS = HO // ROWS_PER_BANK
+HALF_ROWS = H // CORE_BANKS
 G_COLS = P * TAPS
 
+KW_ORDER = (1, 0, 2)
 VECTOR_C = 64
 Y_VECTOR_ROWS = 10
 G_BUFS = 4
+LATE = 2
 
 FLOPS = 2 * TAPS * CO * CI * IMAGES * HO * WO
 BYTES = 2 * IMAGES * CO * HO * WO + 2 * CO * CI * TAPS + 4 * IMAGES * CI * H * W
@@ -53,15 +56,14 @@ def tile_model_pa_kernel(tc, image_in, grad_output, grad_out, out):
         g_scales = keep.tile([P, PASSES, TAPS, CI], U8, align_bytes=64)
         col_codes = keep.tile([P, PASSES, 2, KH, P], U32, align_bytes=64)
         col_scales = keep.tile([P, PASSES, 2, KH, P], U8, align_bytes=64)
+        identity = keep.tile([P, P], F32)
         images = [keep.tile([P, IMAGES, H, W], F32, name="image%d" % ct) for ct in range(C_TILES)]
 
         def copy_to_image(ct, dst, src):
-            if ct < C_TILES // 2:
+            if ct < C_TILES - LATE:
                 nc.scalar.copy(out=dst, in_=src)
             else:
                 nc.vector.tensor_copy(out=dst, in_=src)
-
-        identity = keep.tile([P, P], F32)
 
         y_views = ((y_codes[:].bitcast(I32), IMAGES), (y_scales[:].bitcast(I32), 1))
         col_views = (col_codes[:].bitcast(I32), col_scales[:].bitcast(I32))
@@ -112,17 +114,46 @@ def tile_model_pa_kernel(tc, image_in, grad_output, grad_out, out):
             )
             return y_grouped
 
-        def quantise_y(kp, y_grouped):
-            inner = slice(GROUP, (HO + 1) * GROUP)
-            nc.vector.quantize_mx(
-                out=y_codes[:, kp, 1, inner].bitcast(E4M3_X4),
-                scales=y_scales[:, kp, 1, inner],
-                in_=y_grouped[:].rearrange("p x n t -> p (x n t)"),
-            )
-            for view, slot in y_views:
-                middle = y_rows(view, slot, kp, 1)
-                nc.vector.tensor_copy(out=y_rows(view, slot, kp, 0)[:, :, : (WO - 1) * slot], in_=middle[:, :, slot:])
-                nc.vector.tensor_copy(out=y_rows(view, slot, kp, 2)[:, :, slot:], in_=middle[:, :, : (WO - 1) * slot])
+        def regroup_g(g_raw):
+            g_grouped = g_mid.tile([P, TAPS, P, PACK], BF16, align_bytes=64, name="g_grouped")
+            turned = g_raw[:].rearrange("p t (c x) -> p c x t", x=TAPS)
+            for kh in range(KH):
+                taps = slice(kh * KW, (kh + 1) * KW)
+                regions = g_grouped[:, taps].rearrange("p x c t -> p c x t")
+                nc.vector.tensor_copy(out=regions[:, :VECTOR_C], in_=turned[:, :VECTOR_C, taps])
+                nc.scalar.copy(out=regions[:, VECTOR_C:], in_=turned[:, VECTOR_C:, taps])
+            return g_grouped
+
+        def regroup(kp, ct):
+            y_grouped = regroup_y(kp, raws["y", kp]) if ct == 0 else None
+            return y_grouped, regroup_g(raws[kp, ct])
+
+        def quantise(kp, ct, grouped):
+            y_grouped, g_grouped = grouped
+            if y_grouped is not None:
+                inner = slice(GROUP, (HO + 1) * GROUP)
+                nc.vector.quantize_mx(
+                    out=y_codes[:, kp, 1, inner].bitcast(E4M3_X4),
+                    scales=y_scales[:, kp, 1, inner],
+                    in_=y_grouped[:].rearrange("p x n t -> p (x n t)"),
+                )
+            for kw in KW_ORDER:
+                if y_grouped is not None and kw != 1:
+                    for view, slot in y_views:
+                        kept = (WO - 1) * slot
+                        middle = y_rows(view, slot, kp, 1)
+                        moved = y_rows(view, slot, kp, kw)
+                        if kw == 0:
+                            nc.vector.tensor_copy(out=moved[:, :, :kept], in_=middle[:, :, slot:])
+                        else:
+                            nc.vector.tensor_copy(out=moved[:, :, slot:], in_=middle[:, :, :kept])
+                for kh in range(KH):
+                    tap = kh * KW + kw
+                    nc.vector.quantize_mx(
+                        out=g_codes[:, kp, tap, ct * P : (ct + 1) * P].bitcast(E5M2_X4),
+                        scales=g_scales[:, kp, tap, ct * P : (ct + 1) * P],
+                        in_=g_grouped[:, tap].rearrange("p c t -> p (c t)"),
+                    )
 
         def prepare_columns():
             for (view, slot), cols in zip(y_views, col_views):
@@ -137,47 +168,32 @@ def tile_model_pa_kernel(tc, image_in, grad_output, grad_out, out):
                             in_=middle[:, :, :, u, :],
                         )
 
-        def regroup_g(g_raw):
-            g_grouped = g_mid.tile([P, TAPS, P, PACK], BF16, align_bytes=64, name="g_grouped")
-            turned = g_raw[:].rearrange("p t (c x) -> p c x t", x=TAPS)
-            for kh in range(KH):
-                taps = slice(kh * KW, (kh + 1) * KW)
-                regions = g_grouped[:, taps].rearrange("p x c t -> p c x t")
-                nc.vector.tensor_copy(out=regions[:, :VECTOR_C], in_=turned[:, :VECTOR_C, taps])
-                nc.scalar.copy(out=regions[:, VECTOR_C:], in_=turned[:, VECTOR_C:, taps])
-            return g_grouped
+        banks = {}
 
-        def quantise_g(kp, ct, g_grouped):
-            for tap in range(TAPS):
-                nc.vector.quantize_mx(
-                    out=g_codes[:, kp, tap, ct * P : (ct + 1) * P].bitcast(E5M2_X4),
-                    scales=g_scales[:, kp, tap, ct * P : (ct + 1) * P],
-                    in_=g_grouped[:, tap].rearrange("p c t -> p (c t)"),
-                )
-
-        def core_passes(ct, kp, kh, banks):
-            for kw in range(KW):
-                tap = kh * KW + kw
-                for b in range(CORE_BANKS):
+        def core_passes(kp, ct, b):
+            if kp == 0:
+                banks[ct, b] = psum.tile([P, BANK], F32, name="core", tag="bank%d" % (ct * CORE_BANKS + b))
+            for kw in KW_ORDER:
+                for kh in range(KH):
+                    tap = kh * KW + kw
                     first = (b * ROWS_PER_BANK + 2 - kh) * GROUP
                     nc.tensor.matmul_mx(
-                        out=banks[b][:],
+                        out=banks[ct, b][:],
                         lhsT=g_codes[:, kp, tap, ct * P : (ct + 1) * P].bitcast(E5M2_X4),
                         lhsT_scale=g_scales[:, kp, tap, ct * P : (ct + 1) * P],
                         rhs=y_codes[:, kp, kw, first : first + BANK].bitcast(E4M3_X4),
                         rhs_scale=y_scales[:, kp, kw, first : first + BANK],
-                        start=(kp == 0 and tap == 0),
-                        stop=(kp == PASSES - 1 and tap == TAPS - 1),
+                        start=(kp == 0 and kw == KW_ORDER[0] and kh == 0),
+                        stop=(kp == PASSES - 1 and kw == KW_ORDER[-1] and kh == KH - 1),
                     )
 
-        def core_out(ct, banks):
-            for b in range(CORE_BANKS):
-                top = 1 + b * ROWS_PER_BANK
-                copy_to_image(
-                    ct,
-                    dst=images[ct][:, :, top : top + ROWS_PER_BANK, 1 : 1 + WO],
-                    src=banks[b][:].rearrange("c (r u n) -> c n r u", u=WO, n=IMAGES),
-                )
+        def core_out(ct, b):
+            top = 1 + b * ROWS_PER_BANK
+            copy_to_image(
+                ct,
+                dst=images[ct][:, :, top : top + ROWS_PER_BANK, 1 : 1 + WO],
+                src=banks[ct, b][:].rearrange("c (r u n) -> c n r u", u=WO, n=IMAGES),
+            )
 
         def edge_pass(bank, codes, scales, kp, tap, start, stop):
             nc.tensor.matmul_mx(
@@ -190,63 +206,41 @@ def tile_model_pa_kernel(tc, image_in, grad_output, grad_out, out):
                 stop=stop,
             )
 
-        def store(ct):
+        def store(ct, b):
+            rows = slice(b * HALF_ROWS, (b + 1) * HALF_ROWS)
             nc.sync.dma_start(
-                out=out[:, ct * P : (ct + 1) * P].rearrange("n c h w -> c n (h w)"),
-                in_=images[ct][:].rearrange("c n h w -> c n (h w)"),
+                out=out[:, ct * P : (ct + 1) * P, rows].rearrange("n c h w -> c n (h w)"),
+                in_=images[ct][:, :, rows].rearrange("c n h w -> c n (h w)"),
             )
 
-        chunks = [(kp, pair + ct) for pair in range(0, C_TILES, 2) for kp in range(PASSES) for ct in range(2)]
+        chunks = [(kp, ct) for kp in range(PASSES) for ct in range(C_TILES)]
         raws = {}
-        for kp in range(PASSES):
-            raws["y", kp] = load_y(kp)
-            for ct in range(2):
-                raws[kp, ct] = load_g(kp, ct)
+        raws["y", 0] = load_y(0)
+        for index in range(G_BUFS):
+            raws[chunks[index]] = load_g(*chunks[index])
+        raws["y", 1] = load_y(1)
 
-        def regroup(kp, ct):
-            y_grouped = regroup_y(kp, raws["y", kp]) if ct == 0 else None
-            return y_grouped, regroup_g(raws[kp, ct])
-
-        def quantise(kp, ct, grouped):
-            y_grouped, g_grouped = grouped
-            if ct == 0:
-                quantise_y(kp, y_grouped)
-            quantise_g(kp, ct, g_grouped)
-
-        banks = {}
-
-        def core(kp, ct):
-            if kp == 0:
-                banks[ct] = [psum.tile([P, BANK], F32, name="core%d%d" % (ct % 2, b)) for b in range(CORE_BANKS)]
-            for kh in range(KH):
-                core_passes(ct, kp, kh, banks[ct])
-
-        quantise_y(0, regroup_y(0, raws["y", 0]))
-        quantise_g(0, 0, regroup_g(raws[0, 0]))
-        core(0, 0)
-        grouped = regroup(*chunks[1])
-        full = None
-        for index in range(1, len(chunks) - 1):
-            kp, ct = chunks[index]
-            if index + G_BUFS - 1 < len(chunks):
-                raws[chunks[index + G_BUFS - 1]] = load_g(*chunks[index + G_BUFS - 1])
-            following = regroup(*chunks[index + 1])
-            if full is not None:
-                core_out(full, banks[full])
-                full = None
-            quantise(kp, ct, grouped)
+        grouped = regroup(*chunks[0])
+        for index, (kp, ct) in enumerate(chunks):
+            if index == 0:
+                quantise(kp, ct, grouped)
+            following = regroup(*chunks[index + 1]) if index + 1 < len(chunks) else None
+            if index > 0:
+                quantise(kp, ct, grouped)
             grouped = following
-            core(kp, ct)
-            if kp == PASSES - 1:
-                full = ct
-        last_kp, last_ct = chunks[-1]
-        quantise(last_kp, last_ct, grouped)
+            if index + G_BUFS < len(chunks):
+                raws[chunks[index + G_BUFS]] = load_g(*chunks[index + G_BUFS])
+            if index < len(chunks) - LATE:
+                for b in range(CORE_BANKS):
+                    core_passes(kp, ct, b)
         prepare_columns()
-        core_out(full, banks[full])
+        for ct in range(C_TILES - LATE):
+            for b in range(CORE_BANKS):
+                core_out(ct, b)
 
-        rows_bank = psum.tile([P, BANK], F32, name="rows_bank", tag="edge0")
-        left_bank = psum.tile([P, BANK], F32, name="left_bank", tag="edge1")
-        right_bank = psum.tile([P, BANK], F32, name="right_bank", tag="edge2")
+        rows_bank = psum.tile([P, BANK], F32, name="rows_bank", tag="bank0")
+        left_bank = psum.tile([P, BANK], F32, name="left_bank", tag="bank1")
+        right_bank = psum.tile([P, BANK], F32, name="right_bank", tag="bank2")
         for kp in range(PASSES):
             for kh, first in ((KH - 1, HO * GROUP), (0, 0)):
                 for kw in range(KW):
@@ -277,16 +271,6 @@ def tile_model_pa_kernel(tc, image_in, grad_output, grad_out, out):
             nc.vector.tensor_copy(out=edge[:], in_=bank[:])
             edges.append(edge)
 
-        core_passes(last_ct, last_kp, 0, banks[last_ct])
-        flips = []
-        for ct in range(C_TILES):
-            flip = psum.tile([P, len(edges), P], F32, name="flip%d" % ct, tag="edge%d" % ct)
-            for e, edge in enumerate(edges):
-                nc.tensor.transpose(flip[:, e, :], edge[:, ct * P : (ct + 1) * P], identity[:])
-            flips.append(flip)
-        for kh in range(1, KH):
-            core_passes(last_ct, last_kp, kh, banks[last_ct])
-
         def rim_out(ct):
             for half, p in enumerate((H - 1, 0)):
                 copy_to_image(
@@ -300,8 +284,20 @@ def tile_model_pa_kernel(tc, image_in, grad_output, grad_out, out):
                 src=flips[ct][:, 1:, : H * IMAGES].rearrange("c e (p n) -> c n p e", n=IMAGES),
             )
 
-        for ct in (0, 2, 1, 3):
-            rim_out(ct)
-            if ct == last_ct:
-                core_out(ct, banks[ct])
-            store(ct)
+        late_banks = [(kp, ct, b) for kp, ct in chunks[len(chunks) - LATE :] for b in range(CORE_BANKS)]
+        flips = []
+        for index, (kp, ct, b) in enumerate(late_banks):
+            core_passes(kp, ct, b)
+            core_out(ct, b)
+            if index == 0:
+                for c_tile in range(C_TILES):
+                    flip = psum.tile([P, len(edges), P], F32, name="flip", tag="bank%d" % c_tile)
+                    for e, edge in enumerate(edges):
+                        nc.tensor.transpose(flip[:, e, :], edge[:, c_tile * P : (c_tile + 1) * P], identity[:])
+                    flips.append(flip)
+                for c_tile in range(C_TILES):
+                    rim_out(c_tile)
+                for c_tile in range(C_TILES - LATE):
+                    for half in range(CORE_BANKS):
+                        store(c_tile, half)
+            store(ct, b)

@@ -37,9 +37,12 @@ G_COLS = P * TAPS
 
 KW_ORDER = (1, 0, 2)
 VECTOR_C = 64
-Y_VECTOR_ROWS = 10
+Y_SCALAR_IMAGES = (2,)
 G_BUFS = 4
+MID_BUFS = 5
+AHEAD = 2
 LATE = 2
+FILL = 3
 
 FLOPS = 2 * TAPS * CO * CI * IMAGES * HO * WO
 BYTES = 2 * IMAGES * CO * HO * WO + 2 * CO * CI * TAPS + 4 * IMAGES * CI * H * W
@@ -48,7 +51,7 @@ BYTES = 2 * IMAGES * CO * HO * WO + 2 * CO * CI * TAPS + 4 * IMAGES * CI * H * W
 def tile_model_pa_kernel(tc, image_in, grad_output, grad_out, out):
     nc = tc.nc
     with tc.tile_pool(name="keep", bufs=1) as keep, tc.tile_pool(name="g_in", bufs=G_BUFS) as g_in, tc.tile_pool(
-        name="g_mid", bufs=3
+        name="g_mid", bufs=MID_BUFS
     ) as g_mid, tc.psum_pool(name="psum", bufs=1) as psum, tc.manual_schedule():
         y_codes = keep.tile([P, PASSES, KW, Y_COLS], U32, align_bytes=64)
         y_scales = keep.tile([P, PASSES, KW, Y_COLS], U8, align_bytes=64)
@@ -84,12 +87,15 @@ def tile_model_pa_kernel(tc, image_in, grad_output, grad_out, out):
         make_identity(nc, identity[:])
 
         def load_y(kp):
-            y_raw = keep.tile([P, IMAGES, PACK, HO * WO], BF16, name="y_raw%d" % kp)
-            nc.sync.dma_start(
-                out=y_raw[:].rearrange("p n t x -> p n (t x)"),
-                in_=grad_output[:, kp * K_PASS : (kp + 1) * K_PASS].rearrange("n (p t) i j -> p n (t i j)", t=PACK),
-            )
-            return y_raw
+            tiles = []
+            for n in range(IMAGES):
+                y_raw = keep.tile([P, PACK, HO * WO], BF16, name="y_raw%d_%d" % (kp, n))
+                nc.sync.dma_start(
+                    out=y_raw[:].rearrange("p t x -> p (t x)"),
+                    in_=grad_output[n, kp * K_PASS : (kp + 1) * K_PASS].rearrange("(p t) i j -> p (t i j)", t=PACK),
+                )
+                tiles.append(y_raw)
+            return tiles
 
         def load_g(kp, ct):
             g_raw = g_in.tile([P, PACK, G_COLS], BF16, name="g_raw")
@@ -101,59 +107,49 @@ def tile_model_pa_kernel(tc, image_in, grad_output, grad_out, out):
             )
             return g_raw
 
-        def regroup_y(kp, y_raw):
+        def regroup_y(kp, y_raws):
             y_grouped = keep.tile([P, HO * WO, IMAGES, PACK], BF16, align_bytes=64, name="y_grouped%d" % kp)
-            split = Y_VECTOR_ROWS * WO
-            nc.vector.tensor_copy(
-                out=y_grouped[:, :split].rearrange("p x n t -> p n x t"),
-                in_=y_raw[:, :, :, :split].rearrange("p n t x -> p n x t"),
-            )
-            nc.scalar.copy(
-                out=y_grouped[:, split:].rearrange("p x n t -> p n x t"),
-                in_=y_raw[:, :, :, split:].rearrange("p n t x -> p n x t"),
-            )
+            for n in range(IMAGES):
+                if n in Y_SCALAR_IMAGES:
+                    nc.scalar.copy(out=y_grouped[:, :, n, :], in_=y_raws[n][:].rearrange("p t x -> p x t"))
+                else:
+                    nc.vector.tensor_copy(out=y_grouped[:, :, n, :], in_=y_raws[n][:].rearrange("p t x -> p x t"))
             return y_grouped
 
-        def regroup_g(g_raw):
-            g_grouped = g_mid.tile([P, TAPS, P, PACK], BF16, align_bytes=64, name="g_grouped")
+        def regroup_g(g_raw, kw):
+            g_grouped = g_mid.tile([P, KH, P, PACK], BF16, align_bytes=64, name="g_grouped")
             turned = g_raw[:].rearrange("p t (c x) -> p c x t", x=TAPS)
-            for kh in range(KH):
-                taps = slice(kh * KW, (kh + 1) * KW)
-                regions = g_grouped[:, taps].rearrange("p x c t -> p c x t")
-                nc.vector.tensor_copy(out=regions[:, :VECTOR_C], in_=turned[:, :VECTOR_C, taps])
-                nc.scalar.copy(out=regions[:, VECTOR_C:], in_=turned[:, VECTOR_C:, taps])
+            regions = g_grouped[:].rearrange("p x c t -> p c x t")
+            nc.vector.tensor_copy(out=regions[:, :VECTOR_C], in_=turned[:, :VECTOR_C, kw:TAPS:KW])
+            nc.scalar.copy(out=regions[:, VECTOR_C:], in_=turned[:, VECTOR_C:, kw:TAPS:KW])
             return g_grouped
 
-        def regroup(kp, ct):
-            y_grouped = regroup_y(kp, raws["y", kp]) if ct == 0 else None
-            return y_grouped, regroup_g(raws[kp, ct])
+        def quantise_y(kp, y_grouped):
+            inner = slice(GROUP, (HO + 1) * GROUP)
+            nc.vector.quantize_mx(
+                out=y_codes[:, kp, 1, inner].bitcast(E4M3_X4),
+                scales=y_scales[:, kp, 1, inner],
+                in_=y_grouped[:].rearrange("p x n t -> p (x n t)"),
+            )
 
-        def quantise(kp, ct, grouped):
-            y_grouped, g_grouped = grouped
-            if y_grouped is not None:
-                inner = slice(GROUP, (HO + 1) * GROUP)
+        def shift_y(kp, kw):
+            for view, slot in y_views:
+                kept = (WO - 1) * slot
+                middle = y_rows(view, slot, kp, 1)
+                moved = y_rows(view, slot, kp, kw)
+                if kw == 0:
+                    nc.vector.tensor_copy(out=moved[:, :, :kept], in_=middle[:, :, slot:])
+                else:
+                    nc.vector.tensor_copy(out=moved[:, :, slot:], in_=middle[:, :, :kept])
+
+        def quantise_g(kp, ct, kw, g_grouped):
+            for kh in range(KH):
+                tap = kh * KW + kw
                 nc.vector.quantize_mx(
-                    out=y_codes[:, kp, 1, inner].bitcast(E4M3_X4),
-                    scales=y_scales[:, kp, 1, inner],
-                    in_=y_grouped[:].rearrange("p x n t -> p (x n t)"),
+                    out=g_codes[:, kp, tap, ct * P : (ct + 1) * P].bitcast(E5M2_X4),
+                    scales=g_scales[:, kp, tap, ct * P : (ct + 1) * P],
+                    in_=g_grouped[:, kh].rearrange("p c t -> p (c t)"),
                 )
-            for kw in KW_ORDER:
-                if y_grouped is not None and kw != 1:
-                    for view, slot in y_views:
-                        kept = (WO - 1) * slot
-                        middle = y_rows(view, slot, kp, 1)
-                        moved = y_rows(view, slot, kp, kw)
-                        if kw == 0:
-                            nc.vector.tensor_copy(out=moved[:, :, :kept], in_=middle[:, :, slot:])
-                        else:
-                            nc.vector.tensor_copy(out=moved[:, :, slot:], in_=middle[:, :, :kept])
-                for kh in range(KH):
-                    tap = kh * KW + kw
-                    nc.vector.quantize_mx(
-                        out=g_codes[:, kp, tap, ct * P : (ct + 1) * P].bitcast(E5M2_X4),
-                        scales=g_scales[:, kp, tap, ct * P : (ct + 1) * P],
-                        in_=g_grouped[:, tap].rearrange("p c t -> p (c t)"),
-                    )
 
         def prepare_columns():
             for (view, slot), cols in zip(y_views, col_views):
@@ -170,22 +166,21 @@ def tile_model_pa_kernel(tc, image_in, grad_output, grad_out, out):
 
         banks = {}
 
-        def core_passes(kp, ct, b):
-            if kp == 0:
+        def core_pass(kp, ct, b, kh, kw):
+            first_pass = kp == 0 and kw == KW_ORDER[0] and kh == 0
+            if first_pass:
                 banks[ct, b] = psum.tile([P, BANK], F32, name="core", tag="bank%d" % (ct * CORE_BANKS + b))
-            for kw in KW_ORDER:
-                for kh in range(KH):
-                    tap = kh * KW + kw
-                    first = (b * ROWS_PER_BANK + 2 - kh) * GROUP
-                    nc.tensor.matmul_mx(
-                        out=banks[ct, b][:],
-                        lhsT=g_codes[:, kp, tap, ct * P : (ct + 1) * P].bitcast(E5M2_X4),
-                        lhsT_scale=g_scales[:, kp, tap, ct * P : (ct + 1) * P],
-                        rhs=y_codes[:, kp, kw, first : first + BANK].bitcast(E4M3_X4),
-                        rhs_scale=y_scales[:, kp, kw, first : first + BANK],
-                        start=(kp == 0 and kw == KW_ORDER[0] and kh == 0),
-                        stop=(kp == PASSES - 1 and kw == KW_ORDER[-1] and kh == KH - 1),
-                    )
+            tap = kh * KW + kw
+            first = (b * ROWS_PER_BANK + 2 - kh) * GROUP
+            nc.tensor.matmul_mx(
+                out=banks[ct, b][:],
+                lhsT=g_codes[:, kp, tap, ct * P : (ct + 1) * P].bitcast(E5M2_X4),
+                lhsT_scale=g_scales[:, kp, tap, ct * P : (ct + 1) * P],
+                rhs=y_codes[:, kp, kw, first : first + BANK].bitcast(E4M3_X4),
+                rhs_scale=y_scales[:, kp, kw, first : first + BANK],
+                start=first_pass,
+                stop=(kp == PASSES - 1 and kw == KW_ORDER[-1] and kh == KH - 1),
+            )
 
         def core_out(ct, b):
             top = 1 + b * ROWS_PER_BANK
@@ -206,33 +201,51 @@ def tile_model_pa_kernel(tc, image_in, grad_output, grad_out, out):
                 stop=stop,
             )
 
-        def store(ct, b):
-            rows = slice(b * HALF_ROWS, (b + 1) * HALF_ROWS)
+        def store(ct, top, rows):
             nc.sync.dma_start(
-                out=out[:, ct * P : (ct + 1) * P, rows].rearrange("n c h w -> c n (h w)"),
-                in_=images[ct][:, :, rows].rearrange("c n h w -> c n (h w)"),
+                out=out[:, ct * P : (ct + 1) * P, top : top + rows].rearrange("n c h w -> c n (h w)"),
+                in_=images[ct][:, :, top : top + rows].rearrange("c n h w -> c n (h w)"),
             )
 
         chunks = [(kp, ct) for kp in range(PASSES) for ct in range(C_TILES)]
+        units = [(kp, ct, kw) for kp, ct in chunks for kw in KW_ORDER]
+        second = len(units) // PASSES
+        y_raws = {0: load_y(0)}
         raws = {}
-        raws["y", 0] = load_y(0)
         for index in range(G_BUFS):
             raws[chunks[index]] = load_g(*chunks[index])
-        raws["y", 1] = load_y(1)
+        y_raws[1] = load_y(1)
 
-        grouped = regroup(*chunks[0])
-        for index, (kp, ct) in enumerate(chunks):
-            if index == 0:
-                quantise(kp, ct, grouped)
-            following = regroup(*chunks[index + 1]) if index + 1 < len(chunks) else None
-            if index > 0:
-                quantise(kp, ct, grouped)
-            grouped = following
-            if index + G_BUFS < len(chunks):
-                raws[chunks[index + G_BUFS]] = load_g(*chunks[index + G_BUFS])
-            if index < len(chunks) - LATE:
+        y_grouped = regroup_y(0, y_raws[0])
+        quantise_y(0, y_grouped)
+        shift_y(0, KW_ORDER[1])
+
+        grouped = {}
+        regrouped = 0
+        for index, (kp, ct, kw) in enumerate(units):
+            upto = min(index + min(index, AHEAD), len(units) - 1)
+            while regrouped <= upto:
+                unit = units[regrouped]
+                grouped[unit] = regroup_g(raws[unit[0], unit[1]], unit[2])
+                following = chunks.index((unit[0], unit[1])) + G_BUFS
+                if unit[2] == KW_ORDER[-1] and following < len(chunks):
+                    raws[chunks[following]] = load_g(*chunks[following])
+                regrouped += 1
+            quantise_g(kp, ct, kw, grouped[kp, ct, kw])
+            if index == 1:
+                shift_y(0, KW_ORDER[2])
+            if index == second - 4:
+                y_grouped = regroup_y(1, y_raws[1])
+            if index == second - 2:
+                quantise_y(1, y_grouped)
+            if index == second - 1:
+                shift_y(1, KW_ORDER[1])
+            if index == second:
+                shift_y(1, KW_ORDER[2])
+            if index < len(units) - LATE * KW:
                 for b in range(CORE_BANKS):
-                    core_passes(kp, ct, b)
+                    for kh in range(KH):
+                        core_pass(kp, ct, b, kh, kw)
         prepare_columns()
         for ct in range(C_TILES - LATE):
             for b in range(CORE_BANKS):
@@ -268,8 +281,13 @@ def tile_model_pa_kernel(tc, image_in, grad_output, grad_out, out):
         edges = []
         for e, bank in enumerate((rows_bank, left_bank, right_bank)):
             edge = keep.tile([P, CI], F32, name="edge%d" % e)
-            nc.vector.tensor_copy(out=edge[:], in_=bank[:])
+            if e == 1:
+                nc.scalar.copy(out=edge[:], in_=bank[:])
+            else:
+                nc.vector.tensor_copy(out=edge[:], in_=bank[:])
             edges.append(edge)
+
+        flips = []
 
         def rim_out(ct):
             for half, p in enumerate((H - 1, 0)):
@@ -285,19 +303,19 @@ def tile_model_pa_kernel(tc, image_in, grad_output, grad_out, out):
             )
 
         late_banks = [(kp, ct, b) for kp, ct in chunks[len(chunks) - LATE :] for b in range(CORE_BANKS)]
-        flips = []
+        taps = [(kh, kw) for kw in KW_ORDER for kh in range(KH)]
         for index, (kp, ct, b) in enumerate(late_banks):
-            core_passes(kp, ct, b)
+            for position, (kh, kw) in enumerate(taps):
+                if index == 0 and position == FILL:
+                    for c_tile in range(C_TILES):
+                        flip = psum.tile([P, len(edges), P], F32, name="flip", tag="bank%d" % c_tile)
+                        for e, edge in enumerate(edges):
+                            nc.tensor.transpose(flip[:, e, :], edge[:, c_tile * P : (c_tile + 1) * P], identity[:])
+                        flips.append(flip)
+                    for c_tile in range(C_TILES):
+                        rim_out(c_tile)
+                    for c_tile in range(C_TILES - LATE):
+                        store(c_tile, 0, H)
+                core_pass(kp, ct, b, kh, kw)
             core_out(ct, b)
-            if index == 0:
-                for c_tile in range(C_TILES):
-                    flip = psum.tile([P, len(edges), P], F32, name="flip", tag="bank%d" % c_tile)
-                    for e, edge in enumerate(edges):
-                        nc.tensor.transpose(flip[:, e, :], edge[:, c_tile * P : (c_tile + 1) * P], identity[:])
-                    flips.append(flip)
-                for c_tile in range(C_TILES):
-                    rim_out(c_tile)
-                for c_tile in range(C_TILES - LATE):
-                    for half in range(CORE_BANKS):
-                        store(c_tile, half)
-            store(ct, b)
+            store(ct, b * HALF_ROWS, HALF_ROWS)

@@ -116,12 +116,16 @@ def tile_model_pa_kernel(tc, image_in, grad_output, grad_out, out):
                     nc.vector.tensor_copy(out=y_grouped[:, :, n, :], in_=y_raws[n][:].rearrange("p t x -> p x t"))
             return y_grouped
 
-        def regroup_g(g_raw, kw):
-            g_grouped = g_mid.tile([P, KH, P, PACK], BF16, align_bytes=64, name="g_grouped")
-            turned = g_raw[:].rearrange("p t (c x) -> p c x t", x=TAPS)
+        def regroup_g(g_raws, kw):
+            g_grouped = g_mid.tile([P, KH, len(g_raws) * P, PACK], BF16, align_bytes=64, name="g_grouped")
+            turned = [g_raw[:].rearrange("p t (c x) -> p c x t", x=TAPS)[:, :, kw:TAPS:KW] for g_raw in g_raws]
             regions = g_grouped[:].rearrange("p x c t -> p c x t")
-            nc.vector.tensor_copy(out=regions[:, :VECTOR_C], in_=turned[:, :VECTOR_C, kw:TAPS:KW])
-            nc.scalar.copy(out=regions[:, VECTOR_C:], in_=turned[:, VECTOR_C:, kw:TAPS:KW])
+            if len(g_raws) == 1:
+                nc.vector.tensor_copy(out=regions[:, :VECTOR_C], in_=turned[0][:, :VECTOR_C])
+                nc.scalar.copy(out=regions[:, VECTOR_C:], in_=turned[0][:, VECTOR_C:])
+            else:
+                nc.vector.tensor_copy(out=regions[:, :P], in_=turned[0])
+                nc.scalar.copy(out=regions[:, P:], in_=turned[1])
             return g_grouped
 
         def quantise_y(kp, y_grouped):
@@ -142,12 +146,13 @@ def tile_model_pa_kernel(tc, image_in, grad_output, grad_out, out):
                 else:
                     nc.vector.tensor_copy(out=moved[:, :, slot:], in_=middle[:, :, :kept])
 
-        def quantise_g(kp, ct, kw, g_grouped):
+        def quantise_g(kp, cts, kw, g_grouped):
+            columns = slice(cts[0] * P, (cts[-1] + 1) * P)
             for kh in range(KH):
                 tap = kh * KW + kw
                 nc.vector.quantize_mx(
-                    out=g_codes[:, kp, tap, ct * P : (ct + 1) * P].bitcast(E5M2_X4),
-                    scales=g_scales[:, kp, tap, ct * P : (ct + 1) * P],
+                    out=g_codes[:, kp, tap, columns].bitcast(E5M2_X4),
+                    scales=g_scales[:, kp, tap, columns],
                     in_=g_grouped[:, kh].rearrange("p c t -> p (c t)"),
                 )
 
@@ -208,8 +213,9 @@ def tile_model_pa_kernel(tc, image_in, grad_output, grad_out, out):
             )
 
         chunks = [(kp, ct) for kp in range(PASSES) for ct in range(C_TILES)]
-        units = [(kp, ct, kw) for kp, ct in chunks for kw in KW_ORDER]
-        second = len(units) // PASSES
+        groups = [(0, (0,)), (0, (1,)), (0, (2, 3)), (1, (0, 1)), (1, (2, 3))]
+        units = [(kp, cts, kw) for kp, cts in groups for kw in KW_ORDER]
+        second = units.index((1, (0, 1), KW_ORDER[0]))
         y_raws = {0: load_y(0)}
         raws = {}
         for index in range(G_BUFS):
@@ -222,19 +228,20 @@ def tile_model_pa_kernel(tc, image_in, grad_output, grad_out, out):
 
         grouped = {}
         regrouped = 0
-        for index, (kp, ct, kw) in enumerate(units):
+        for index, (kp, cts, kw) in enumerate(units):
             upto = min(index + min(index, AHEAD), len(units) - 1)
             while regrouped <= upto:
                 unit = units[regrouped]
-                grouped[unit] = regroup_g(raws[unit[0], unit[1]], unit[2])
-                following = chunks.index((unit[0], unit[1])) + G_BUFS
-                if unit[2] == KW_ORDER[-1] and following < len(chunks):
-                    raws[chunks[following]] = load_g(*chunks[following])
+                grouped[unit] = regroup_g([raws[unit[0], ct] for ct in unit[1]], unit[2])
+                for ct in unit[1]:
+                    following = chunks.index((unit[0], ct)) + G_BUFS
+                    if unit[2] == KW_ORDER[-1] and following < len(chunks):
+                        raws[chunks[following]] = load_g(*chunks[following])
                 regrouped += 1
-            quantise_g(kp, ct, kw, grouped[kp, ct, kw])
+            quantise_g(kp, cts, kw, grouped[kp, cts, kw])
             if index == 1:
                 shift_y(0, KW_ORDER[2])
-            if index == second - 4:
+            if index == second - 3:
                 y_grouped = regroup_y(1, y_raws[1])
             if index == second - 2:
                 quantise_y(1, y_grouped)
@@ -242,10 +249,11 @@ def tile_model_pa_kernel(tc, image_in, grad_output, grad_out, out):
                 shift_y(1, KW_ORDER[1])
             if index == second:
                 shift_y(1, KW_ORDER[2])
-            if index < len(units) - LATE * KW:
-                for b in range(CORE_BANKS):
-                    for kh in range(KH):
-                        core_pass(kp, ct, b, kh, kw)
+            if index < len(units) - KW:
+                for ct in cts:
+                    for b in range(CORE_BANKS):
+                        for kh in range(KH):
+                            core_pass(kp, ct, b, kh, kw)
         prepare_columns()
         for ct in range(C_TILES - LATE):
             for b in range(CORE_BANKS):

@@ -41,6 +41,7 @@ Y_SCALAR_IMAGES = (2,)
 G_BUFS = 4
 MID_BUFS = 5
 AHEAD = 2
+START_AHEAD = (0, 1, 0, 1)
 LATE = 2
 FILL = 3
 
@@ -229,7 +230,8 @@ def tile_model_pa_kernel(tc, image_in, grad_output, grad_out, out):
         grouped = {}
         regrouped = 0
         for index, (kp, cts, kw) in enumerate(units):
-            upto = min(index + min(index, AHEAD), len(units) - 1)
+            ahead = START_AHEAD[index] if index < len(START_AHEAD) else AHEAD
+            upto = min(index + ahead, len(units) - 1)
             while regrouped <= upto:
                 unit = units[regrouped]
                 grouped[unit] = regroup_g([raws[unit[0], ct] for ct in unit[1]], unit[2])
@@ -249,12 +251,13 @@ def tile_model_pa_kernel(tc, image_in, grad_output, grad_out, out):
                 shift_y(1, KW_ORDER[1])
             if index == second:
                 shift_y(1, KW_ORDER[2])
+            if index == second + 1:
+                prepare_columns()
             if index < len(units) - KW:
                 for ct in cts:
                     for b in range(CORE_BANKS):
                         for kh in range(KH):
                             core_pass(kp, ct, b, kh, kw)
-        prepare_columns()
         for ct in range(C_TILES - LATE):
             for b in range(CORE_BANKS):
                 core_out(ct, b)
@@ -262,38 +265,35 @@ def tile_model_pa_kernel(tc, image_in, grad_output, grad_out, out):
         rows_bank = psum.tile([P, BANK], F32, name="rows_bank", tag="bank0")
         left_bank = psum.tile([P, BANK], F32, name="left_bank", tag="bank1")
         right_bank = psum.tile([P, BANK], F32, name="right_bank", tag="bank2")
+        sides = {0: (0, left_bank), KW - 1: (1, right_bank)}
         for kp in range(PASSES):
-            for kh, first in ((KH - 1, HO * GROUP), (0, 0)):
-                for kw in range(KW):
+            for kw in KW_ORDER:
+                for kh, first in ((KH - 1, HO * GROUP), (0, 0)):
                     edge_pass(
                         rows_bank,
                         y_codes[:, kp, kw, first : first + P],
                         y_scales[:, kp, kw, first : first + P],
                         kp,
                         kh * KW + kw,
-                        start=(kp == 0 and kh == KH - 1 and kw == 0),
-                        stop=(kp == PASSES - 1 and kh == 0 and kw == KW - 1),
+                        start=(kp == 0 and kw == KW_ORDER[0] and kh == KH - 1),
+                        stop=(kp == PASSES - 1 and kw == KW_ORDER[-1] and kh == 0),
                     )
-        for side, (bank, kw) in enumerate(((left_bank, 0), (right_bank, KW - 1))):
-            for kp in range(PASSES):
-                for kh in range(KH):
-                    edge_pass(
-                        bank,
-                        col_codes[:, kp, side, kh, :],
-                        col_scales[:, kp, side, kh, :],
-                        kp,
-                        kh * KW + kw,
-                        start=(kp == 0 and kh == 0),
-                        stop=(kp == PASSES - 1 and kh == KH - 1),
-                    )
-        edges = []
-        for e, bank in enumerate((rows_bank, left_bank, right_bank)):
-            edge = keep.tile([P, CI], F32, name="edge%d" % e)
-            if e == 1:
-                nc.scalar.copy(out=edge[:], in_=bank[:])
-            else:
-                nc.vector.tensor_copy(out=edge[:], in_=bank[:])
-            edges.append(edge)
+                if kw in sides:
+                    side, bank = sides[kw]
+                    for kh in range(KH):
+                        edge_pass(
+                            bank,
+                            col_codes[:, kp, side, kh, :],
+                            col_scales[:, kp, side, kh, :],
+                            kp,
+                            kh * KW + kw,
+                            start=(kp == 0 and kh == 0),
+                            stop=(kp == PASSES - 1 and kh == KH - 1),
+                        )
+        edges = [keep.tile([P, CI], F32, name="edge%d" % e) for e in range(3)]
+        nc.scalar.copy(out=edges[1][:], in_=left_bank[:])
+        nc.vector.tensor_copy(out=edges[0][:], in_=rows_bank[:])
+        nc.vector.tensor_copy(out=edges[2][:], in_=right_bank[:])
 
         flips = []
 

@@ -39,9 +39,9 @@ KW_ORDER = (1, 0, 2)
 VECTOR_C = 64
 Y_SCALAR_IMAGES = (2,)
 G_BUFS = 4
-MID_BUFS = 5
-AHEAD = 2
-START_AHEAD = (0, 1, 0, 1)
+MID_BUFS = 4
+AHEAD = 1
+START_AHEAD = (0, 1, 0)
 LATE = 2
 FILL = 3
 
@@ -108,14 +108,16 @@ def tile_model_pa_kernel(tc, image_in, grad_output, grad_out, out):
             )
             return g_raw
 
-        def regroup_y(kp, y_raws):
-            y_grouped = keep.tile([P, HO * WO, IMAGES, PACK], BF16, align_bytes=64, name="y_grouped%d" % kp)
-            for n in range(IMAGES):
+        y_groupeds = [
+            keep.tile([P, HO * WO, IMAGES, PACK], BF16, align_bytes=64, name="y_grouped%d" % kp) for kp in range(PASSES)
+        ]
+
+        def regroup_y(kp, some_images):
+            for n in some_images:
                 if n in Y_SCALAR_IMAGES:
-                    nc.scalar.copy(out=y_grouped[:, :, n, :], in_=y_raws[n][:].rearrange("p t x -> p x t"))
+                    nc.scalar.copy(out=y_groupeds[kp][:, :, n, :], in_=y_raws[kp][n][:].rearrange("p t x -> p x t"))
                 else:
-                    nc.vector.tensor_copy(out=y_grouped[:, :, n, :], in_=y_raws[n][:].rearrange("p t x -> p x t"))
-            return y_grouped
+                    nc.vector.tensor_copy(out=y_groupeds[kp][:, :, n, :], in_=y_raws[kp][n][:].rearrange("p t x -> p x t"))
 
         def regroup_g(g_raws, kw):
             g_grouped = g_mid.tile([P, KH, len(g_raws) * P, PACK], BF16, align_bytes=64, name="g_grouped")
@@ -129,12 +131,12 @@ def tile_model_pa_kernel(tc, image_in, grad_output, grad_out, out):
                 nc.scalar.copy(out=regions[:, P:], in_=turned[1])
             return g_grouped
 
-        def quantise_y(kp, y_grouped):
+        def quantise_y(kp):
             inner = slice(GROUP, (HO + 1) * GROUP)
             nc.vector.quantize_mx(
                 out=y_codes[:, kp, 1, inner].bitcast(E4M3_X4),
                 scales=y_scales[:, kp, 1, inner],
-                in_=y_grouped[:].rearrange("p x n t -> p (x n t)"),
+                in_=y_groupeds[kp][:].rearrange("p x n t -> p (x n t)"),
             )
 
         def shift_y(kp, kw):
@@ -223,8 +225,8 @@ def tile_model_pa_kernel(tc, image_in, grad_output, grad_out, out):
             raws[chunks[index]] = load_g(*chunks[index])
         y_raws[1] = load_y(1)
 
-        y_grouped = regroup_y(0, y_raws[0])
-        quantise_y(0, y_grouped)
+        regroup_y(0, range(IMAGES))
+        quantise_y(0)
         shift_y(0, KW_ORDER[1])
 
         grouped = {}
@@ -244,23 +246,27 @@ def tile_model_pa_kernel(tc, image_in, grad_output, grad_out, out):
             if index == 1:
                 shift_y(0, KW_ORDER[2])
             if index == second - 3:
-                y_grouped = regroup_y(1, y_raws[1])
+                regroup_y(1, (0,))
             if index == second - 2:
-                quantise_y(1, y_grouped)
+                regroup_y(1, (1, 2))
             if index == second - 1:
-                shift_y(1, KW_ORDER[1])
+                regroup_y(1, (3,))
+                quantise_y(1)
             if index == second:
-                shift_y(1, KW_ORDER[2])
+                shift_y(1, KW_ORDER[1])
             if index == second + 1:
+                shift_y(1, KW_ORDER[2])
+            if index == second + 2:
                 prepare_columns()
+            if index == len(units) - 3:
+                for early in range(C_TILES - LATE):
+                    for b in range(CORE_BANKS):
+                        core_out(early, b)
             if index < len(units) - KW:
                 for ct in cts:
                     for b in range(CORE_BANKS):
                         for kh in range(KH):
                             core_pass(kp, ct, b, kh, kw)
-        for ct in range(C_TILES - LATE):
-            for b in range(CORE_BANKS):
-                core_out(ct, b)
 
         rows_bank = psum.tile([P, BANK], F32, name="rows_bank", tag="bank0")
         left_bank = psum.tile([P, BANK], F32, name="left_bank", tag="bank1")

@@ -44,6 +44,7 @@ AHEAD = 1
 START_AHEAD = (0, 1, 0)
 LATE = 2
 FILL = 3
+END_IMAGES = 2
 
 FLOPS = 2 * TAPS * CO * CI * IMAGES * HO * WO
 BYTES = 2 * IMAGES * CO * HO * WO + 2 * CO * CI * TAPS + 4 * IMAGES * CI * H * W
@@ -190,12 +191,12 @@ def tile_model_pa_kernel(tc, image_in, grad_output, grad_out, out):
                 stop=(kp == PASSES - 1 and kw == KW_ORDER[-1] and kh == KH - 1),
             )
 
-        def core_out(ct, b):
+        def core_out(ct, b, some=slice(0, IMAGES)):
             top = 1 + b * ROWS_PER_BANK
             copy_to_image(
                 ct,
-                dst=images[ct][:, :, top : top + ROWS_PER_BANK, 1 : 1 + WO],
-                src=banks[ct, b][:].rearrange("c (r u n) -> c n r u", u=WO, n=IMAGES),
+                dst=images[ct][:, some, top : top + ROWS_PER_BANK, 1 : 1 + WO],
+                src=banks[ct, b][:].rearrange("c (r u n) -> c n r u", u=WO, n=IMAGES)[:, some],
             )
 
         def edge_pass(bank, codes, scales, kp, tap, start, stop):
@@ -209,10 +210,10 @@ def tile_model_pa_kernel(tc, image_in, grad_output, grad_out, out):
                 stop=stop,
             )
 
-        def store(ct, top, rows):
+        def store(ct, top, rows, some=slice(0, IMAGES)):
             nc.sync.dma_start(
-                out=out[:, ct * P : (ct + 1) * P, top : top + rows].rearrange("n c h w -> c n (h w)"),
-                in_=images[ct][:, :, top : top + rows].rearrange("c n h w -> c n (h w)"),
+                out=out[some, ct * P : (ct + 1) * P, top : top + rows].rearrange("n c h w -> c n (h w)"),
+                in_=images[ct][:, some, top : top + rows].rearrange("c n h w -> c n (h w)"),
             )
 
         chunks = [(kp, ct) for kp in range(PASSES) for ct in range(C_TILES)]
@@ -331,5 +332,7 @@ def tile_model_pa_kernel(tc, image_in, grad_output, grad_out, out):
                     for c_tile in range(C_TILES - LATE):
                         store(c_tile, 0, H)
                 core_pass(kp, ct, b, kh, kw)
-            core_out(ct, b)
-            store(ct, b * HALF_ROWS, HALF_ROWS)
+            step = END_IMAGES if index == len(late_banks) - 1 else IMAGES
+            for n in range(0, IMAGES, step):
+                core_out(ct, b, slice(n, n + step))
+                store(ct, b * HALF_ROWS, HALF_ROWS, slice(n, n + step))

@@ -8,12 +8,14 @@ U32 = mybir.dt.uint32
 U8 = mybir.dt.uint8
 E4M3_X4 = mybir.dt.float8_e4m3fn_x4
 E5M2_X4 = mybir.dt.float8_e5m2_x4
+ADD = mybir.AluOpType.add
 
 P = 128
 PACK = 4
 K_PASS = P * PACK
-
 IMAGES = 4
+PAIRS = 2
+M = 2
 CI = 512
 CO = 1024
 HO = 16
@@ -27,24 +29,26 @@ PASSES = CO // K_PASS
 C_TILES = CI // P
 BANK = 512
 
-GROUP = WO * IMAGES
-Y_GROUPS = HO + 2
+HALVES = 2
+R = HO // HALVES
+SLOT = HALVES * M
+GROUP = WO * SLOT
+Y_GROUPS = R + 2
 Y_COLS = Y_GROUPS * GROUP
-ROWS_PER_BANK = BANK // GROUP
-CORE_BANKS = HO // ROWS_PER_BANK
-HALF_ROWS = H // CORE_BANKS
 G_COLS = P * TAPS
 
+SEG = WO * IMAGES
+SEGS = 12
+EDGES = 4
+
 KW_ORDER = (1, 0, 2)
-VECTOR_C = 64
-Y_SCALAR_IMAGES = (2,)
-G_BUFS = 4
-MID_BUFS = 4
-AHEAD = 1
-START_AHEAD = (0, 1, 0)
+KH_ORDER = (1, 0, 2)
+FIRST_C = 64
+FIRST_CUT = 40
+LONE_CUT = 64
+PAIR_CUT = 160
 LATE = 2
 FILL = 3
-END_IMAGES = 2
 
 FLOPS = 2 * TAPS * CO * CI * IMAGES * HO * WO
 BYTES = 2 * IMAGES * CO * HO * WO + 2 * CO * CI * TAPS + 4 * IMAGES * CI * H * W
@@ -52,99 +56,104 @@ BYTES = 2 * IMAGES * CO * HO * WO + 2 * CO * CI * TAPS + 4 * IMAGES * CI * H * W
 
 def tile_model_pa_kernel(tc, image_in, grad_output, grad_out, out):
     nc = tc.nc
-    with tc.tile_pool(name="keep", bufs=1) as keep, tc.tile_pool(name="g_in", bufs=G_BUFS) as g_in, tc.tile_pool(
-        name="g_mid", bufs=MID_BUFS
+    with tc.tile_pool(name="keep", bufs=1) as keep, tc.tile_pool(name="y_in", bufs=2) as y_in, tc.tile_pool(
+        name="g_mid", bufs=4
     ) as g_mid, tc.psum_pool(name="psum", bufs=1) as psum, tc.manual_schedule():
-        y_codes = keep.tile([P, PASSES, KW, Y_COLS], U32, align_bytes=64)
-        y_scales = keep.tile([P, PASSES, KW, Y_COLS], U8, align_bytes=64)
+        y_codes = keep.tile([P, PASSES, PAIRS, KW, Y_COLS], U32, align_bytes=64)
+        y_scales = keep.tile([P, PASSES, PAIRS, KW, Y_COLS], U8, align_bytes=64)
         g_codes = keep.tile([P, PASSES, TAPS, CI], U32, align_bytes=64)
         g_scales = keep.tile([P, PASSES, TAPS, CI], U8, align_bytes=64)
-        col_codes = keep.tile([P, PASSES, 2, KH, P], U32, align_bytes=64)
-        col_scales = keep.tile([P, PASSES, 2, KH, P], U8, align_bytes=64)
+        rim_codes = keep.tile([P, PASSES, SEGS, SEG], U32, align_bytes=64)
+        rim_scales = keep.tile([P, PASSES, SEGS, SEG], U8, align_bytes=64)
         identity = keep.tile([P, P], F32)
         images = [keep.tile([P, IMAGES, H, W], F32, name="image%d" % ct) for ct in range(C_TILES)]
 
-        def copy_to_image(ct, dst, src):
-            if ct < C_TILES - LATE:
-                nc.scalar.copy(out=dst, in_=src)
-            else:
-                nc.vector.tensor_copy(out=dst, in_=src)
+        y_words = ((y_codes[:].bitcast(I32), SLOT), (y_scales[:].bitcast(I32), 1))
+        y_single = ((y_codes[:].bitcast(I32), rim_codes[:].bitcast(I32)), (y_scales[:], rim_scales[:]))
 
-        y_views = ((y_codes[:].bitcast(I32), IMAGES), (y_scales[:].bitcast(I32), 1))
-        col_views = (col_codes[:].bitcast(I32), col_scales[:].bitcast(I32))
-
-        def y_rows(view, slot, kp, kw):
+        for view, slot in y_words:
             width = WO * slot
-            return view[:, kp, kw, width : (HO + 1) * width].rearrange("p (i c) -> p i c", c=width)
-
-        for view, slot in y_views:
-            width = WO * slot
-            nc.vector.memset(view[:, :, :, :width], 0)
-            nc.vector.memset(view[:, :, :, (HO + 1) * width :], 0)
+            nc.vector.memset(view[:, :, :, 1, :width], 0)
+            nc.vector.memset(view[:, :, :, 1, (Y_GROUPS - 1) * width :], 0)
             for kp in range(PASSES):
-                nc.vector.memset(y_rows(view, slot, kp, 0)[:, :, width - slot :], 0)
-                nc.vector.memset(y_rows(view, slot, kp, 2)[:, :, :slot], 0)
-        nc.gpsimd.memset(col_codes[:].bitcast(F32), 0.0)
-        nc.gpsimd.memset(col_scales[:].bitcast(F32), 0.0)
+                for kw, column in ((0, WO - 1), (2, 0)):
+                    nc.vector.memset(
+                        view[:, kp, :, kw, :].rearrange("p r (g c) -> p r g c", c=width)[
+                            :, :, :, column * slot : (column + 1) * slot
+                        ],
+                        0,
+                    )
+        for image in images:
+            nc.vector.memset(image[:, :, 0, 16:18], 0.0)
+            nc.vector.memset(image[:, :, 17, 0:2], 0.0)
+        nc.gpsimd.memset(rim_codes[:].bitcast(F32), 0.0)
+        nc.gpsimd.memset(rim_scales[:].bitcast(F32), 0.0)
         make_identity(nc, identity[:])
 
-        def load_y(kp):
-            tiles = []
-            for n in range(IMAGES):
-                y_raw = keep.tile([P, PACK, HO * WO], BF16, name="y_raw%d_%d" % (kp, n))
-                nc.sync.dma_start(
-                    out=y_raw[:].rearrange("p t x -> p (t x)"),
-                    in_=grad_output[n, kp * K_PASS : (kp + 1) * K_PASS].rearrange("(p t) i j -> p (t i j)", t=PACK),
-                )
-                tiles.append(y_raw)
-            return tiles
+        def load_y(kp, pr):
+            y_raw = y_in.tile([P, M, PACK * HO * WO], BF16, name="y_raw")
+            nc.sync.dma_start(
+                out=y_raw[:],
+                in_=grad_output[pr * M : (pr + 1) * M, kp * K_PASS : (kp + 1) * K_PASS].rearrange(
+                    "n (p t) i j -> p n (t i j)", t=PACK
+                ),
+            )
+            return y_raw
 
-        def load_g(kp, ct):
-            g_raw = g_in.tile([P, PACK, G_COLS], BF16, name="g_raw")
+        def load_g(kp, first, count):
+            g_raw = keep.tile([P, PACK, count * TAPS], BF16, name="g_raw_%d_%d" % (kp, first))
             nc.sync.dma_start(
                 out=g_raw[:],
-                in_=grad_out[kp * K_PASS : (kp + 1) * K_PASS, ct * P : (ct + 1) * P].rearrange(
+                in_=grad_out[kp * K_PASS : (kp + 1) * K_PASS, first : first + count].rearrange(
                     "(p t) c kh kw -> p t (c kh kw)", t=PACK
                 ),
             )
             return g_raw
 
-        y_groupeds = [
-            keep.tile([P, HO * WO, IMAGES, PACK], BF16, align_bytes=64, name="y_grouped%d" % kp) for kp in range(PASSES)
-        ]
-
-        def regroup_y(kp, some_images):
-            for n in some_images:
-                if n in Y_SCALAR_IMAGES:
-                    nc.scalar.copy(out=y_groupeds[kp][:, :, n, :], in_=y_raws[kp][n][:].rearrange("p t x -> p x t"))
-                else:
-                    nc.vector.tensor_copy(out=y_groupeds[kp][:, :, n, :], in_=y_raws[kp][n][:].rearrange("p t x -> p x t"))
-
-        def regroup_g(g_raws, kw):
-            g_grouped = g_mid.tile([P, KH, len(g_raws) * P, PACK], BF16, align_bytes=64, name="g_grouped")
-            turned = [g_raw[:].rearrange("p t (c x) -> p c x t", x=TAPS)[:, :, kw:TAPS:KW] for g_raw in g_raws]
-            regions = g_grouped[:].rearrange("p x c t -> p c x t")
-            if len(g_raws) == 1:
-                nc.vector.tensor_copy(out=regions[:, :VECTOR_C], in_=turned[0][:, :VECTOR_C])
-                nc.scalar.copy(out=regions[:, VECTOR_C:], in_=turned[0][:, VECTOR_C:])
+        def regroup_y(kp, pr, h, grouped):
+            dst = grouped[:].rearrange("p (a b h m) t -> p h a m b t", b=4, h=HALVES, m=M)[:, h]
+            src = y_raws[kp, pr][:].rearrange("p m (t h a b) -> p h a m b t", t=PACK, h=HALVES, b=4)[:, h]
+            if h == 0:
+                nc.vector.tensor_copy(out=dst, in_=src)
             else:
-                nc.vector.tensor_copy(out=regions[:, :P], in_=turned[0])
-                nc.scalar.copy(out=regions[:, P:], in_=turned[1])
+                nc.scalar.copy(out=dst, in_=src)
+
+        def new_grouped():
+            y_grouped = y_in.tile([P, BANK, PACK], BF16, align_bytes=64, name="y_grouped")
+            return y_grouped
+
+        def regroup_g(g_raw, kw, g_grouped, first, cut):
+            turned = g_raw[:].rearrange("p t (c x) -> p c x t", x=TAPS)[:, :, kw:TAPS:KW]
+            count = g_raw.shape[2] // TAPS
+            regions = g_grouped[:].rearrange("p x c t -> p c x t")[:, first : first + count]
+            if cut > 0:
+                nc.vector.tensor_copy(out=regions[:, :cut], in_=turned[:, :cut])
+            if cut < count:
+                nc.scalar.copy(out=regions[:, cut:], in_=turned[:, cut:])
+
+        def new_g_grouped(cts):
+            g_grouped = g_mid.tile([P, KH, len(cts) * P, PACK], BF16, align_bytes=64, name="g_grouped")
             return g_grouped
 
-        def quantise_y(kp):
-            inner = slice(GROUP, (HO + 1) * GROUP)
+        def quantise_y(kp, pr, grouped):
             nc.vector.quantize_mx(
-                out=y_codes[:, kp, 1, inner].bitcast(E4M3_X4),
-                scales=y_scales[:, kp, 1, inner],
-                in_=y_groupeds[kp][:].rearrange("p x n t -> p (x n t)"),
+                out=y_codes[:, kp, pr, 1, GROUP : GROUP + BANK].bitcast(E4M3_X4),
+                scales=y_scales[:, kp, pr, 1, GROUP : GROUP + BANK],
+                in_=grouped[:].rearrange("p x t -> p (x t)"),
             )
 
-        def shift_y(kp, kw):
-            for view, slot in y_views:
-                kept = (WO - 1) * slot
-                middle = y_rows(view, slot, kp, 1)
-                moved = y_rows(view, slot, kp, kw)
+        def halo_y(kp, pr):
+            for view, ribbon in y_single:
+                groups = view[:, kp, pr, 1, :].rearrange("p (g u h m) -> p g u h m", u=WO, h=HALVES, m=M)
+                nc.vector.tensor_copy(out=groups[:, 0, :, 1, :], in_=groups[:, R, :, 0, :])
+                nc.vector.tensor_copy(out=groups[:, R + 1, :, 0, :], in_=groups[:, 1, :, 1, :])
+
+        def shift_y(kp, pr, kw):
+            for view, slot in y_words:
+                width = WO * slot
+                kept = width - slot
+                middle = view[:, kp, pr, 1, :].rearrange("p (g c) -> p g c", c=width)
+                moved = view[:, kp, pr, kw, :].rearrange("p (g c) -> p g c", c=width)
                 if kw == 0:
                     nc.vector.tensor_copy(out=moved[:, :, :kept], in_=middle[:, :, slot:])
                 else:
@@ -152,7 +161,7 @@ def tile_model_pa_kernel(tc, image_in, grad_output, grad_out, out):
 
         def quantise_g(kp, cts, kw, g_grouped):
             columns = slice(cts[0] * P, (cts[-1] + 1) * P)
-            for kh in range(KH):
+            for kh in KH_ORDER:
                 tap = kh * KW + kw
                 nc.vector.quantize_mx(
                     out=g_codes[:, kp, tap, columns].bitcast(E5M2_X4),
@@ -160,179 +169,235 @@ def tile_model_pa_kernel(tc, image_in, grad_output, grad_out, out):
                     in_=g_grouped[:, kh].rearrange("p c t -> p (c t)"),
                 )
 
-        def prepare_columns():
-            for (view, slot), cols in zip(y_views, col_views):
-                width = WO * slot
-                middle = view[:, :, 1, width : (HO + 1) * width].rearrange("p k (i u s) -> p k i u s", u=WO, s=slot)
-                for side, u in enumerate((0, WO - 1)):
-                    for kh in range(KH):
-                        nc.vector.tensor_copy(
-                            out=cols[:, :, side, kh, kh * slot : (kh + HO) * slot].rearrange(
-                                "p k (i s) -> p k i s", s=slot
-                            ),
-                            in_=middle[:, :, :, u, :],
-                        )
+        def rim_rows():
+            for view, ribbon in y_single:
+                middle = view[:, :, :, 1, :].rearrange("p k r (g u h m) -> p k r g h u m", u=WO, h=HALVES, m=M)
+                for seg, g, h, src_u, dst_u in (
+                    (1, 1, 0, slice(0, 16), slice(0, 16)),
+                    (11, 1, 0, slice(0, 15), slice(1, 16)),
+                    (7, R, 1, slice(0, 16), slice(0, 16)),
+                    (5, R, 1, slice(1, 16), slice(0, 15)),
+                ):
+                    nc.vector.tensor_copy(
+                        out=ribbon[:, :, seg].rearrange("p k (u r m) -> p k r u m", r=PAIRS, m=M)[:, :, :, dst_u],
+                        in_=middle[:, :, :, g, h, src_u],
+                    )
+
+        def rim_columns(kp):
+            for view, ribbon in y_single:
+                middle = view[:, kp, :, 1, :].rearrange("p r (g u h m) -> p u r h g m", u=WO, h=HALVES, m=M)
+                for seg, u, g in ((4, 0, 1), (2, 0, 2), (10, WO - 1, 1), (8, WO - 1, 0)):
+                    nc.vector.tensor_copy(
+                        out=ribbon[:, kp, seg].rearrange("p (h g r m) -> p r h g m", h=HALVES, r=PAIRS, m=M),
+                        in_=middle[:, u, :, :, g : g + R],
+                    )
 
         banks = {}
 
-        def core_pass(kp, ct, b, kh, kw):
-            first_pass = kp == 0 and kw == KW_ORDER[0] and kh == 0
+        def core_pass(kp, ct, pr, kh, kw):
+            first_pass = kp == 0 and kw == KW_ORDER[0] and kh == KH_ORDER[0]
             if first_pass:
-                banks[ct, b] = psum.tile([P, BANK], F32, name="core", tag="bank%d" % (ct * CORE_BANKS + b))
+                banks[ct, pr] = psum.tile([P, BANK], F32, name="core", tag="bank%d" % (ct * PAIRS + pr))
             tap = kh * KW + kw
-            first = (b * ROWS_PER_BANK + 2 - kh) * GROUP
+            first = (2 - kh) * GROUP
             nc.tensor.matmul_mx(
-                out=banks[ct, b][:],
+                out=banks[ct, pr][:],
                 lhsT=g_codes[:, kp, tap, ct * P : (ct + 1) * P].bitcast(E5M2_X4),
                 lhsT_scale=g_scales[:, kp, tap, ct * P : (ct + 1) * P],
-                rhs=y_codes[:, kp, kw, first : first + BANK].bitcast(E4M3_X4),
-                rhs_scale=y_scales[:, kp, kw, first : first + BANK],
+                rhs=y_codes[:, kp, pr, kw, first : first + BANK].bitcast(E4M3_X4),
+                rhs_scale=y_scales[:, kp, pr, kw, first : first + BANK],
                 start=first_pass,
-                stop=(kp == PASSES - 1 and kw == KW_ORDER[-1] and kh == KH - 1),
+                stop=(kp == PASSES - 1 and kw == KW_ORDER[-1] and kh == KH_ORDER[-1]),
             )
 
-        def core_out(ct, b, some=slice(0, IMAGES)):
-            top = 1 + b * ROWS_PER_BANK
-            copy_to_image(
-                ct,
-                dst=images[ct][:, some, top : top + ROWS_PER_BANK, 1 : 1 + WO],
-                src=banks[ct, b][:].rearrange("c (r u n) -> c n r u", u=WO, n=IMAGES)[:, some],
+        def core_out(ct, pr, m, copy):
+            copy(
+                out=images[ct][:, pr * M + m, 1 : 1 + HO, 1 : 1 + WO].rearrange("c (h r) w -> c h r w", h=HALVES),
+                in_=banks[ct, pr][:].rearrange("c (r u h m) -> c m h r u", u=WO, h=HALVES, m=M)[:, m],
             )
 
-        def edge_pass(bank, codes, scales, kp, tap, start, stop):
+        def edge_pass(bank, kp, seg, tap, start, stop):
+            flat_codes = rim_codes[:, kp].rearrange("p s c -> p (s c)")
+            flat_scales = rim_scales[:, kp].rearrange("p s c -> p (s c)")
             nc.tensor.matmul_mx(
                 out=bank[:],
-                lhsT=codes.bitcast(E4M3_X4),
-                lhsT_scale=scales,
+                lhsT=flat_codes[:, seg * SEG : (seg + 2) * SEG].bitcast(E4M3_X4),
+                lhsT_scale=flat_scales[:, seg * SEG : (seg + 2) * SEG],
                 rhs=g_codes[:, kp, tap, :].bitcast(E5M2_X4),
                 rhs_scale=g_scales[:, kp, tap, :],
                 start=start,
                 stop=stop,
             )
 
-        def store(ct, top, rows, some=slice(0, IMAGES)):
+        def store(ct, n, count):
             nc.sync.dma_start(
-                out=out[some, ct * P : (ct + 1) * P, top : top + rows].rearrange("n c h w -> c n (h w)"),
-                in_=images[ct][:, some, top : top + rows].rearrange("c n h w -> c n (h w)"),
+                out=out[n : n + count, ct * P : (ct + 1) * P].rearrange("n c h w -> c n (h w)"),
+                in_=images[ct][:, n : n + count].rearrange("c n h w -> c n (h w)"),
             )
 
-        chunks = [(kp, ct) for kp in range(PASSES) for ct in range(C_TILES)]
         groups = [(0, (0,)), (0, (1,)), (0, (2, 3)), (1, (0, 1)), (1, (2, 3))]
         units = [(kp, cts, kw) for kp, cts in groups for kw in KW_ORDER]
         second = units.index((1, (0, 1), KW_ORDER[0]))
-        y_raws = {0: load_y(0)}
+        y_raws = {}
         raws = {}
-        for index in range(G_BUFS):
-            raws[chunks[index]] = load_g(*chunks[index])
-        y_raws[1] = load_y(1)
+        y_raws[0, 0] = load_y(0, 0)
+        halves = [load_g(0, first, FIRST_C) for first in range(0, P, FIRST_C)]
+        y_raws[0, 1] = load_y(0, 1)
+        for kp, cts in groups[1:3]:
+            raws[kp, cts] = load_g(kp, cts[0] * P, len(cts) * P)
 
-        regroup_y(0, range(IMAGES))
-        quantise_y(0)
-        shift_y(0, KW_ORDER[1])
+        def lone_passes(pr, kw):
+            for kh in KH_ORDER:
+                core_pass(0, 0, pr, kh, kw)
+
+        def regroup_first(kw):
+            for half, cut in enumerate((FIRST_C, 0)):
+                regroup_g(halves[half], kw, grouped[0, (0,), kw], half * FIRST_C, cut)
 
         grouped = {}
-        regrouped = 0
-        for index, (kp, cts, kw) in enumerate(units):
-            ahead = START_AHEAD[index] if index < len(START_AHEAD) else AHEAD
-            upto = min(index + ahead, len(units) - 1)
-            while regrouped <= upto:
+        for unit in units[:3]:
+            grouped[unit] = new_g_grouped(unit[1])
+        y_first = new_grouped()
+        y_second = new_grouped()
+        for h in range(HALVES):
+            regroup_y(0, 0, h, y_first)
+        regroup_g(halves[0], KW_ORDER[0], grouped[units[0]], 0, FIRST_CUT)
+        quantise_y(0, 0, y_first)
+        halo_y(0, 0)
+        regroup_g(halves[1], KW_ORDER[0], grouped[units[0]], FIRST_C, FIRST_CUT)
+        quantise_g(*units[0], grouped[units[0]])
+        lone_passes(0, KW_ORDER[0])
+        shift_y(0, 0, KW_ORDER[1])
+        regroup_first(KW_ORDER[1])
+        for h in range(HALVES):
+            regroup_y(0, 1, h, y_second)
+        for pr in range(PAIRS):
+            y_raws[1, pr] = load_y(1, pr)
+        for kp, cts in groups[3:]:
+            raws[kp, cts] = load_g(kp, cts[0] * P, len(cts) * P)
+        quantise_g(*units[1], grouped[units[1]])
+        lone_passes(0, KW_ORDER[1])
+        quantise_y(0, 1, y_second)
+        halo_y(0, 1)
+        lone_passes(1, KW_ORDER[0])
+        regroup_first(KW_ORDER[2])
+        shift_y(0, 1, KW_ORDER[1])
+        lone_passes(1, KW_ORDER[1])
+        shift_y(0, 0, KW_ORDER[2])
+        quantise_g(*units[2], grouped[units[2]])
+        lone_passes(0, KW_ORDER[2])
+        shift_y(0, 1, KW_ORDER[2])
+        lone_passes(1, KW_ORDER[2])
+
+        y_late = {}
+        regrouped = 3
+        for index in range(3, len(units)):
+            kp, cts, kw = units[index]
+            while regrouped <= min(index + 1, len(units) - 1):
                 unit = units[regrouped]
-                grouped[unit] = regroup_g([raws[unit[0], ct] for ct in unit[1]], unit[2])
-                for ct in unit[1]:
-                    following = chunks.index((unit[0], ct)) + G_BUFS
-                    if unit[2] == KW_ORDER[-1] and following < len(chunks):
-                        raws[chunks[following]] = load_g(*chunks[following])
+                grouped[unit] = new_g_grouped(unit[1])
+                cut = LONE_CUT if len(unit[1]) == 1 else PAIR_CUT
+                regroup_g(raws[unit[0], unit[1]], unit[2], grouped[unit], 0, cut)
                 regrouped += 1
             quantise_g(kp, cts, kw, grouped[kp, cts, kw])
-            if index == 1:
-                shift_y(0, KW_ORDER[2])
             if index == second - 3:
-                regroup_y(1, (0,))
+                y_late[0] = new_grouped()
+                for h in range(HALVES):
+                    regroup_y(1, 0, h, y_late[0])
             if index == second - 2:
-                regroup_y(1, (1, 2))
+                y_late[1] = new_grouped()
+                for h in range(HALVES):
+                    regroup_y(1, 1, h, y_late[1])
+                quantise_y(1, 0, y_late[0])
+                halo_y(1, 0)
             if index == second - 1:
-                regroup_y(1, (3,))
-                quantise_y(1)
+                quantise_y(1, 1, y_late[1])
+                halo_y(1, 1)
             if index == second:
-                shift_y(1, KW_ORDER[1])
+                for pr in range(PAIRS):
+                    shift_y(1, pr, KW_ORDER[1])
             if index == second + 1:
-                shift_y(1, KW_ORDER[2])
+                for pr in range(PAIRS):
+                    shift_y(1, pr, KW_ORDER[2])
             if index == second + 2:
-                prepare_columns()
-            if index == len(units) - 3:
-                for early in range(C_TILES - LATE):
-                    for b in range(CORE_BANKS):
-                        core_out(early, b)
+                rim_rows()
+                for half in range(PASSES):
+                    rim_columns(half)
             if index < len(units) - KW:
                 for ct in cts:
-                    for b in range(CORE_BANKS):
-                        for kh in range(KH):
-                            core_pass(kp, ct, b, kh, kw)
+                    for pr in range(PAIRS):
+                        for kh in KH_ORDER:
+                            core_pass(kp, ct, pr, kh, kw)
 
-        rows_bank = psum.tile([P, BANK], F32, name="rows_bank", tag="bank0")
-        left_bank = psum.tile([P, BANK], F32, name="left_bank", tag="bank1")
-        right_bank = psum.tile([P, BANK], F32, name="right_bank", tag="bank2")
-        sides = {0: (0, left_bank), KW - 1: (1, right_bank)}
-        for kp in range(PASSES):
-            for kw in KW_ORDER:
-                for kh, first in ((KH - 1, HO * GROUP), (0, 0)):
-                    edge_pass(
-                        rows_bank,
-                        y_codes[:, kp, kw, first : first + P],
-                        y_scales[:, kp, kw, first : first + P],
-                        kp,
-                        kh * KW + kw,
-                        start=(kp == 0 and kw == KW_ORDER[0] and kh == KH - 1),
-                        stop=(kp == PASSES - 1 and kw == KW_ORDER[-1] and kh == 0),
-                    )
-                if kw in sides:
-                    side, bank = sides[kw]
-                    for kh in range(KH):
-                        edge_pass(
-                            bank,
-                            col_codes[:, kp, side, kh, :],
-                            col_scales[:, kp, side, kh, :],
-                            kp,
-                            kh * KW + kw,
-                            start=(kp == 0 and kh == 0),
-                            stop=(kp == PASSES - 1 and kh == KH - 1),
-                        )
-        edges = [keep.tile([P, CI], F32, name="edge%d" % e) for e in range(3)]
-        nc.scalar.copy(out=edges[1][:], in_=left_bank[:])
-        nc.vector.tensor_copy(out=edges[0][:], in_=rows_bank[:])
-        nc.vector.tensor_copy(out=edges[2][:], in_=right_bank[:])
+        for ct in range(C_TILES - LATE):
+            for pr in range(PAIRS):
+                for m in range(M):
+                    core_out(ct, pr, m, nc.scalar.copy)
+
+        rim_by_bank = (
+            (0, 1, (0, 0)),
+            (0, 3, (1, 0)),
+            (1, 7, (2, 2)),
+            (1, 9, (1, 2)),
+            (2, 10, (0, 2)),
+            (2, 0, (0, 1)),
+            (3, 6, (2, 1)),
+            (3, 4, (2, 0)),
+        )
+        rim_by_tap = sorted(rim_by_bank, key=lambda part: (KW_ORDER.index(part[2][1]), (0, 3, 2, 1).index(part[0])))
+        edge_banks = [psum.tile([P, BANK], F32, name="edge_bank", tag="bank%d" % e) for e in range(EDGES)]
+        for kp, parts in enumerate((rim_by_bank, rim_by_tap)):
+            for index, (e, seg, (kh, kw)) in enumerate(parts):
+                same = [i for i, other in enumerate(parts) if other[0] == e]
+                edge_pass(
+                    edge_banks[e],
+                    kp,
+                    seg,
+                    kh * KW + kw,
+                    start=(kp == 0 and index == same[0]),
+                    stop=(kp == PASSES - 1 and index == same[-1]),
+                )
+        edges = [keep.tile([P, CI], F32, name="edge%d" % e) for e in range(EDGES)]
+        nc.scalar.copy(out=edges[0][:], in_=edge_banks[0][:])
+        nc.vector.tensor_copy(out=edges[3][:], in_=edge_banks[3][:])
+        nc.scalar.copy(out=edges[2][:], in_=edge_banks[2][:])
+        nc.vector.tensor_copy(out=edges[1][:], in_=edge_banks[1][:])
 
         flips = []
 
         def rim_out(ct):
-            for half, p in enumerate((H - 1, 0)):
-                copy_to_image(
-                    ct,
-                    dst=images[ct][:, :, p, 1 : 1 + WO],
-                    src=flips[ct][:, 0, half * GROUP : (half + 1) * GROUP].rearrange("c (u n) -> c n u", n=IMAGES),
-                )
-            copy_to_image(
-                ct,
-                dst=images[ct][:, :, :, 0 : W : W - 1],
-                src=flips[ct][:, 1:, : H * IMAGES].rearrange("c e (p n) -> c n p e", n=IMAGES),
-            )
+            image = images[ct]
+            rows = [flips[ct][:, e, half * SEG : (half + 1) * SEG].rearrange("c (x n) -> c n x", n=IMAGES) for e in range(EDGES) for half in range(2)]
+            nc.scalar.copy(out=image[:, :, 0, 0:16], in_=rows[0])
+            nc.scalar.copy(out=image[:, :, 1:17, 0], in_=rows[1])
+            nc.scalar.copy(out=image[:, :, 17, 2:18], in_=rows[2])
+            nc.scalar.copy(out=image[:, :, 1:17, 17], in_=rows[3])
+            for place, part in (
+                (image[:, :, 0, 1:17], rows[5]),
+                (image[:, :, 2:18, 0], rows[6]),
+                (image[:, :, 17, 1:17], rows[7]),
+                (image[:, :, 0:16, 17], rows[4]),
+            ):
+                nc.vector.tensor_tensor(out=place, in0=part, in1=place, op=ADD)
 
-        late_banks = [(kp, ct, b) for kp, ct in chunks[len(chunks) - LATE :] for b in range(CORE_BANKS)]
-        taps = [(kh, kw) for kw in KW_ORDER for kh in range(KH)]
-        for index, (kp, ct, b) in enumerate(late_banks):
+        late_banks = [(1, ct, pr) for ct in range(C_TILES - LATE, C_TILES) for pr in range(PAIRS)]
+        taps = [(kh, kw) for kw in KW_ORDER for kh in KH_ORDER]
+        for index, (kp, ct, pr) in enumerate(late_banks):
             for position, (kh, kw) in enumerate(taps):
                 if index == 0 and position == FILL:
                     for c_tile in range(C_TILES):
-                        flip = psum.tile([P, len(edges), P], F32, name="flip", tag="bank%d" % c_tile)
-                        for e, edge in enumerate(edges):
-                            nc.tensor.transpose(flip[:, e, :], edge[:, c_tile * P : (c_tile + 1) * P], identity[:])
+                        flip = psum.tile([P, EDGES, P], F32, name="flip", tag="bank%d" % c_tile)
+                        for e in range(EDGES):
+                            nc.tensor.transpose(flip[:, e, :], edges[e][:, c_tile * P : (c_tile + 1) * P], identity[:])
                         flips.append(flip)
                     for c_tile in range(C_TILES):
                         rim_out(c_tile)
-                    for c_tile in range(C_TILES - LATE):
-                        store(c_tile, 0, H)
-                core_pass(kp, ct, b, kh, kw)
-            step = END_IMAGES if index == len(late_banks) - 1 else IMAGES
-            for n in range(0, IMAGES, step):
-                core_out(ct, b, slice(n, n + step))
-                store(ct, b * HALF_ROWS, HALF_ROWS, slice(n, n + step))
+                        if c_tile < C_TILES - LATE:
+                            store(c_tile, 0, IMAGES)
+                core_pass(kp, ct, pr, kh, kw)
+            for m in range(M):
+                core_out(ct, pr, m, nc.vector.tensor_copy)
+                if index == len(late_banks) - 1:
+                    store(ct, pr * M + m, 1)
+            if index < len(late_banks) - 1:
+                store(ct, pr * M, M)

@@ -111,8 +111,8 @@ def tile_model_pa_kernel(tc, image_in, grad_output, grad_out, out):
             return g_raw
 
         def regroup_y(kp, pr, h, grouped):
-            dst = grouped[:].rearrange("p (a b h m) t -> p h a m b t", b=4, h=HALVES, m=M)[:, h]
-            src = y_raws[kp, pr][:].rearrange("p m (t h a b) -> p h a m b t", t=PACK, h=HALVES, b=4)[:, h]
+            dst = grouped[:].rearrange("p (a b h m) t -> p h a m t b", b=4, h=HALVES, m=M)[:, h]
+            src = y_raws[kp, pr][:].rearrange("p m (t h a b) -> p h a m t b", t=PACK, h=HALVES, b=4)[:, h]
             if h == 0:
                 nc.vector.tensor_copy(out=dst, in_=src)
             else:
@@ -123,13 +123,13 @@ def tile_model_pa_kernel(tc, image_in, grad_output, grad_out, out):
             return y_grouped
 
         def regroup_g(g_raw, kw, g_grouped, first, cut):
-            turned = g_raw[:].rearrange("p t (c x) -> p c x t", x=TAPS)[:, :, kw:TAPS:KW]
             count = g_raw.shape[2] // TAPS
-            regions = g_grouped[:].rearrange("p x c t -> p c x t")[:, first : first + count]
+            turned = g_raw[:].rearrange("p t (b c x) -> p b t x c", c=2, x=TAPS)[:, :, :, kw:TAPS:KW]
+            regions = g_grouped[:, :, first : first + count].rearrange("p x (b c) t -> p b t x c", c=2)
             if cut > 0:
-                nc.vector.tensor_copy(out=regions[:, :cut], in_=turned[:, :cut])
+                nc.vector.tensor_copy(out=regions[:, : cut // 2], in_=turned[:, : cut // 2])
             if cut < count:
-                nc.scalar.copy(out=regions[:, cut:], in_=turned[:, cut:])
+                nc.scalar.copy(out=regions[:, cut // 2 :], in_=turned[:, cut // 2 :])
 
         def new_g_grouped(cts):
             g_grouped = g_mid.tile([P, KH, len(cts) * P, PACK], BF16, align_bytes=64, name="g_grouped")

import concourse.mybir as mybir
from concourse.masks import make_identity

F32 = mybir.dt.float32
BF16 = mybir.dt.bfloat16
I32 = mybir.dt.int32
U32 = mybir.dt.uint32
U8 = mybir.dt.uint8
E4M3_X4 = mybir.dt.float8_e4m3fn_x4
E5M2_X4 = mybir.dt.float8_e5m2_x4
ADD = mybir.AluOpType.add

P = 128
PACK = 4
K_PASS = P * PACK
IMAGES = 4
PAIRS = 2
M = 2
CI = 512
CO = 1024
HO = 16
WO = 16
H = 18
W = 18
KH = 3
KW = 3
TAPS = KH * KW
PASSES = CO // K_PASS
C_TILES = CI // P
BANK = 512

HALVES = 2
R = HO // HALVES
SLOT = HALVES * M
GROUP = WO * SLOT
Y_GROUPS = R + 2
Y_COLS = Y_GROUPS * GROUP
G_COLS = P * TAPS

SEG = WO * IMAGES
SEGS = 12
EDGES = 4

KW_ORDER = (1, 0, 2)
KH_ORDER = (1, 0, 2)
FIRST_C = 64
FIRST_CUT = 40
LONE_CUT = 64
PAIR_CUT = 160
LATE = 2
FILL = 3

FLOPS = 2 * TAPS * CO * CI * IMAGES * HO * WO
BYTES = 2 * IMAGES * CO * HO * WO + 2 * CO * CI * TAPS + 4 * IMAGES * CI * H * W


def tile_model_pa_kernel(tc, image_in, grad_output, grad_out, out):
    nc = tc.nc
    with tc.tile_pool(name="keep", bufs=1) as keep, tc.tile_pool(name="y_in", bufs=2) as y_in, tc.tile_pool(
        name="g_mid", bufs=4
    ) as g_mid, tc.psum_pool(name="psum", bufs=1) as psum, tc.manual_schedule():
        y_codes = keep.tile([P, PASSES, PAIRS, KW, Y_COLS], U32, align_bytes=64)
        y_scales = keep.tile([P, PASSES, PAIRS, KW, Y_COLS], U8, align_bytes=64)
        g_codes = keep.tile([P, PASSES, TAPS, CI], U32, align_bytes=64)
        g_scales = keep.tile([P, PASSES, TAPS, CI], U8, align_bytes=64)
        rim_codes = keep.tile([P, PASSES, SEGS, SEG], U32, align_bytes=64)
        rim_scales = keep.tile([P, PASSES, SEGS, SEG], U8, align_bytes=64)
        identity = keep.tile([P, P], F32)
        images = [keep.tile([P, IMAGES, H, W], F32, name="image%d" % ct) for ct in range(C_TILES)]

        y_words = ((y_codes[:].bitcast(I32), SLOT), (y_scales[:].bitcast(I32), 1))
        y_single = ((y_codes[:].bitcast(I32), rim_codes[:].bitcast(I32)), (y_scales[:], rim_scales[:]))

        for view, slot in y_words:
            width = WO * slot
            nc.vector.memset(view[:, :, :, 1, :width], 0)
            nc.vector.memset(view[:, :, :, 1, (Y_GROUPS - 1) * width :], 0)
            for kp in range(PASSES):
                for kw, column in ((0, WO - 1), (2, 0)):
                    nc.vector.memset(
                        view[:, kp, :, kw, :].rearrange("p r (g c) -> p r g c", c=width)[
                            :, :, :, column * slot : (column + 1) * slot
                        ],
                        0,
                    )
        for image in images:
            nc.vector.memset(image[:, :, 0, 16:18], 0.0)
            nc.vector.memset(image[:, :, 17, 0:2], 0.0)
        nc.gpsimd.memset(rim_codes[:].bitcast(F32), 0.0)
        nc.gpsimd.memset(rim_scales[:].bitcast(F32), 0.0)
        make_identity(nc, identity[:])

        def load_y(kp, pr):
            y_raw = y_in.tile([P, M, PACK * HO * WO], BF16, name="y_raw")
            nc.sync.dma_start(
                out=y_raw[:],
                in_=grad_output[pr * M : (pr + 1) * M, kp * K_PASS : (kp + 1) * K_PASS].rearrange(
                    "n (p t) i j -> p n (t i j)", t=PACK
                ),
            )
            return y_raw

        def load_g(kp, first, count):
            g_raw = keep.tile([P, PACK, count * TAPS], BF16, name="g_raw_%d_%d" % (kp, first))
            nc.sync.dma_start(
                out=g_raw[:],
                in_=grad_out[kp * K_PASS : (kp + 1) * K_PASS, first : first + count].rearrange(
                    "(p t) c kh kw -> p t (c kh kw)", t=PACK
                ),
            )
            return g_raw

        def regroup_y(kp, pr, h, grouped):
            dst = grouped[:].rearrange("p (a b h m) t -> p h a m t b", b=4, h=HALVES, m=M)[:, h]
            src = y_raws[kp, pr][:].rearrange("p m (t h a b) -> p h a m t b", t=PACK, h=HALVES, b=4)[:, h]
            if h == 0:
                nc.vector.tensor_copy(out=dst, in_=src)
            else:
                nc.scalar.copy(out=dst, in_=src)

        def new_grouped():
            y_grouped = y_in.tile([P, BANK, PACK], BF16, align_bytes=64, name="y_grouped")
            return y_grouped

        def regroup_g(g_raw, kw, g_grouped, first, cut):
            count = g_raw.shape[2] // TAPS
            turned = g_raw[:].rearrange("p t (b c x) -> p b t x c", c=2, x=TAPS)[:, :, :, kw:TAPS:KW]
            regions = g_grouped[:, :, first : first + count].rearrange("p x (b c) t -> p b t x c", c=2)
            if cut > 0:
                nc.vector.tensor_copy(out=regions[:, : cut // 2], in_=turned[:, : cut // 2])
            if cut < count:
                nc.scalar.copy(out=regions[:, cut // 2 :], in_=turned[:, cut // 2 :])

        def new_g_grouped(cts):
            g_grouped = g_mid.tile([P, KH, len(cts) * P, PACK], BF16, align_bytes=64, name="g_grouped")
            return g_grouped

        def quantise_y(kp, pr, grouped):
            nc.vector.quantize_mx(
                out=y_codes[:, kp, pr, 1, GROUP : GROUP + BANK].bitcast(E4M3_X4),
                scales=y_scales[:, kp, pr, 1, GROUP : GROUP + BANK],
                in_=grouped[:].rearrange("p x t -> p (x t)"),
            )

        def halo_y(kp, pr):
            for view, ribbon in y_single:
                groups = view[:, kp, pr, 1, :].rearrange("p (g u h m) -> p g u h m", u=WO, h=HALVES, m=M)
                nc.vector.tensor_copy(out=groups[:, 0, :, 1, :], in_=groups[:, R, :, 0, :])
                nc.vector.tensor_copy(out=groups[:, R + 1, :, 0, :], in_=groups[:, 1, :, 1, :])

        def shift_y(kp, pr, kw):
            for view, slot in y_words:
                width = WO * slot
                kept = width - slot
                middle = view[:, kp, pr, 1, :].rearrange("p (g c) -> p g c", c=width)
                moved = view[:, kp, pr, kw, :].rearrange("p (g c) -> p g c", c=width)
                if kw == 0:
                    nc.vector.tensor_copy(out=moved[:, :, :kept], in_=middle[:, :, slot:])
                else:
                    nc.vector.tensor_copy(out=moved[:, :, slot:], in_=middle[:, :, :kept])

        def quantise_g(kp, cts, kw, g_grouped):
            columns = slice(cts[0] * P, (cts[-1] + 1) * P)
            for kh in KH_ORDER:
                tap = kh * KW + kw
                nc.vector.quantize_mx(
                    out=g_codes[:, kp, tap, columns].bitcast(E5M2_X4),
                    scales=g_scales[:, kp, tap, columns],
                    in_=g_grouped[:, kh].rearrange("p c t -> p (c t)"),
                )

        def rim_rows():
            for view, ribbon in y_single:
                middle = view[:, :, :, 1, :].rearrange("p k r (g u h m) -> p k r g h u m", u=WO, h=HALVES, m=M)
                for seg, g, h, src_u, dst_u in (
                    (1, 1, 0, slice(0, 16), slice(0, 16)),
                    (11, 1, 0, slice(0, 15), slice(1, 16)),
                    (7, R, 1, slice(0, 16), slice(0, 16)),
                    (5, R, 1, slice(1, 16), slice(0, 15)),
                ):
                    nc.vector.tensor_copy(
                        out=ribbon[:, :, seg].rearrange("p k (u r m) -> p k r u m", r=PAIRS, m=M)[:, :, :, dst_u],
                        in_=middle[:, :, :, g, h, src_u],
                    )

        def rim_columns(kp):
            for view, ribbon in y_single:
                middle = view[:, kp, :, 1, :].rearrange("p r (g u h m) -> p u r h g m", u=WO, h=HALVES, m=M)
                for seg, u, g in ((4, 0, 1), (2, 0, 2), (10, WO - 1, 1), (8, WO - 1, 0)):
                    nc.vector.tensor_copy(
                        out=ribbon[:, kp, seg].rearrange("p (h g r m) -> p r h g m", h=HALVES, r=PAIRS, m=M),
                        in_=middle[:, u, :, :, g : g + R],
                    )

        banks = {}

        def core_pass(kp, ct, pr, kh, kw):
            first_pass = kp == 0 and kw == KW_ORDER[0] and kh == KH_ORDER[0]
            if first_pass:
                banks[ct, pr] = psum.tile([P, BANK], F32, name="core", tag="bank%d" % (ct * PAIRS + pr))
            tap = kh * KW + kw
            first = (2 - kh) * GROUP
            nc.tensor.matmul_mx(
                out=banks[ct, pr][:],
                lhsT=g_codes[:, kp, tap, ct * P : (ct + 1) * P].bitcast(E5M2_X4),
                lhsT_scale=g_scales[:, kp, tap, ct * P : (ct + 1) * P],
                rhs=y_codes[:, kp, pr, kw, first : first + BANK].bitcast(E4M3_X4),
                rhs_scale=y_scales[:, kp, pr, kw, first : first + BANK],
                start=first_pass,
                stop=(kp == PASSES - 1 and kw == KW_ORDER[-1] and kh == KH_ORDER[-1]),
            )

        def core_out(ct, pr, m, copy):
            copy(
                out=images[ct][:, pr * M + m, 1 : 1 + HO, 1 : 1 + WO].rearrange("c (h r) w -> c h r w", h=HALVES),
                in_=banks[ct, pr][:].rearrange("c (r u h m) -> c m h r u", u=WO, h=HALVES, m=M)[:, m],
            )

        def edge_pass(bank, kp, seg, tap, start, stop):
            flat_codes = rim_codes[:, kp].rearrange("p s c -> p (s c)")
            flat_scales = rim_scales[:, kp].rearrange("p s c -> p (s c)")
            nc.tensor.matmul_mx(
                out=bank[:],
                lhsT=flat_codes[:, seg * SEG : (seg + 2) * SEG].bitcast(E4M3_X4),
                lhsT_scale=flat_scales[:, seg * SEG : (seg + 2) * SEG],
                rhs=g_codes[:, kp, tap, :].bitcast(E5M2_X4),
                rhs_scale=g_scales[:, kp, tap, :],
                start=start,
                stop=stop,
            )

        def store(ct, n, count):
            nc.sync.dma_start(
                out=out[n : n + count, ct * P : (ct + 1) * P].rearrange("n c h w -> c n (h w)"),
                in_=images[ct][:, n : n + count].rearrange("c n h w -> c n (h w)"),
            )

        groups = [(0, (0,)), (0, (1,)), (0, (2, 3)), (1, (0, 1)), (1, (2, 3))]
        units = [(kp, cts, kw) for kp, cts in groups for kw in KW_ORDER]
        second = units.index((1, (0, 1), KW_ORDER[0]))
        y_raws = {}
        raws = {}
        y_raws[0, 0] = load_y(0, 0)
        halves = [load_g(0, first, FIRST_C) for first in range(0, P, FIRST_C)]
        y_raws[0, 1] = load_y(0, 1)
        for kp, cts in groups[1:3]:
            raws[kp, cts] = load_g(kp, cts[0] * P, len(cts) * P)

        def lone_passes(pr, kw):
            for kh in KH_ORDER:
                core_pass(0, 0, pr, kh, kw)

        def regroup_first(kw):
            for half, cut in enumerate((FIRST_C, 0)):
                regroup_g(halves[half], kw, grouped[0, (0,), kw], half * FIRST_C, cut)

        grouped = {}
        for unit in units[:3]:
            grouped[unit] = new_g_grouped(unit[1])
        y_first = new_grouped()
        y_second = new_grouped()
        for h in range(HALVES):
            regroup_y(0, 0, h, y_first)
        regroup_g(halves[0], KW_ORDER[0], grouped[units[0]], 0, FIRST_CUT)
        quantise_y(0, 0, y_first)
        halo_y(0, 0)
        regroup_g(halves[1], KW_ORDER[0], grouped[units[0]], FIRST_C, FIRST_CUT)
        quantise_g(*units[0], grouped[units[0]])
        lone_passes(0, KW_ORDER[0])
        shift_y(0, 0, KW_ORDER[1])
        regroup_first(KW_ORDER[1])
        for h in range(HALVES):
            regroup_y(0, 1, h, y_second)
        for pr in range(PAIRS):
            y_raws[1, pr] = load_y(1, pr)
        for kp, cts in groups[3:]:
            raws[kp, cts] = load_g(kp, cts[0] * P, len(cts) * P)
        quantise_g(*units[1], grouped[units[1]])
        lone_passes(0, KW_ORDER[1])
        quantise_y(0, 1, y_second)
        halo_y(0, 1)
        lone_passes(1, KW_ORDER[0])
        regroup_first(KW_ORDER[2])
        shift_y(0, 1, KW_ORDER[1])
        lone_passes(1, KW_ORDER[1])
        shift_y(0, 0, KW_ORDER[2])
        quantise_g(*units[2], grouped[units[2]])
        lone_passes(0, KW_ORDER[2])
        shift_y(0, 1, KW_ORDER[2])
        lone_passes(1, KW_ORDER[2])

        y_late = {}
        regrouped = 3
        for index in range(3, len(units)):
            kp, cts, kw = units[index]
            while regrouped <= min(index + 1, len(units) - 1):
                unit = units[regrouped]
                grouped[unit] = new_g_grouped(unit[1])
                cut = LONE_CUT if len(unit[1]) == 1 else PAIR_CUT
                regroup_g(raws[unit[0], unit[1]], unit[2], grouped[unit], 0, cut)
                regrouped += 1
            quantise_g(kp, cts, kw, grouped[kp, cts, kw])
            if index == second - 3:
                y_late[0] = new_grouped()
                for h in range(HALVES):
                    regroup_y(1, 0, h, y_late[0])
            if index == second - 2:
                y_late[1] = new_grouped()
                for h in range(HALVES):
                    regroup_y(1, 1, h, y_late[1])
                quantise_y(1, 0, y_late[0])
                halo_y(1, 0)
            if index == second - 1:
                quantise_y(1, 1, y_late[1])
                halo_y(1, 1)
            if index == second:
                for pr in range(PAIRS):
                    shift_y(1, pr, KW_ORDER[1])
            if index == second + 1:
                for pr in range(PAIRS):
                    shift_y(1, pr, KW_ORDER[2])
            if index == second + 2:
                rim_rows()
                for half in range(PASSES):
                    rim_columns(half)
            if index < len(units) - KW:
                for ct in cts:
                    for pr in range(PAIRS):
                        for kh in KH_ORDER:
                            core_pass(kp, ct, pr, kh, kw)

        for ct in range(C_TILES - LATE):
            for pr in range(PAIRS):
                for m in range(M):
                    core_out(ct, pr, m, nc.scalar.copy)

        rim_by_bank = (
            (0, 1, (0, 0)),
            (0, 3, (1, 0)),
            (1, 7, (2, 2)),
            (1, 9, (1, 2)),
            (2, 10, (0, 2)),
            (2, 0, (0, 1)),
            (3, 6, (2, 1)),
            (3, 4, (2, 0)),
        )
        rim_by_tap = sorted(rim_by_bank, key=lambda part: (KW_ORDER.index(part[2][1]), (0, 3, 2, 1).index(part[0])))
        edge_banks = [psum.tile([P, BANK], F32, name="edge_bank", tag="bank%d" % e) for e in range(EDGES)]
        for kp, parts in enumerate((rim_by_bank, rim_by_tap)):
            for index, (e, seg, (kh, kw)) in enumerate(parts):
                same = [i for i, other in enumerate(parts) if other[0] == e]
                edge_pass(
                    edge_banks[e],
                    kp,
                    seg,
                    kh * KW + kw,
                    start=(kp == 0 and index == same[0]),
                    stop=(kp == PASSES - 1 and index == same[-1]),
                )
        edges = [keep.tile([P, CI], F32, name="edge%d" % e) for e in range(EDGES)]
        nc.scalar.copy(out=edges[0][:], in_=edge_banks[0][:])
        nc.vector.tensor_copy(out=edges[3][:], in_=edge_banks[3][:])
        nc.scalar.copy(out=edges[2][:], in_=edge_banks[2][:])
        nc.vector.tensor_copy(out=edges[1][:], in_=edge_banks[1][:])

        flips = []

        def rim_out(ct):
            image = images[ct]
            rows = [flips[ct][:, e, half * SEG : (half + 1) * SEG].rearrange("c (x n) -> c n x", n=IMAGES) for e in range(EDGES) for half in range(2)]
            nc.scalar.copy(out=image[:, :, 0, 0:16], in_=rows[0])
            nc.scalar.copy(out=image[:, :, 1:17, 0], in_=rows[1])
            nc.scalar.copy(out=image[:, :, 17, 2:18], in_=rows[2])
            nc.scalar.copy(out=image[:, :, 1:17, 17], in_=rows[3])
            for place, part in (
                (image[:, :, 0, 1:17], rows[5]),
                (image[:, :, 2:18, 0], rows[6]),
                (image[:, :, 17, 1:17], rows[7]),
                (image[:, :, 0:16, 17], rows[4]),
            ):
                nc.vector.tensor_tensor(out=place, in0=part, in1=place, op=ADD)

        late_banks = [(1, ct, pr) for ct in range(C_TILES - LATE, C_TILES) for pr in range(PAIRS)]
        taps = [(kh, kw) for kw in KW_ORDER for kh in KH_ORDER]
        for index, (kp, ct, pr) in enumerate(late_banks):
            for position, (kh, kw) in enumerate(taps):
                if index == 0 and position == FILL:
                    for c_tile in range(C_TILES):
                        flip = psum.tile([P, EDGES, P], F32, name="flip", tag="bank%d" % c_tile)
                        for e in range(EDGES):
                            nc.tensor.transpose(flip[:, e, :], edges[e][:, c_tile * P : (c_tile + 1) * P], identity[:])
                        flips.append(flip)
                    for c_tile in range(C_TILES):
                        rim_out(c_tile)
                        if c_tile < C_TILES - LATE:
                            store(c_tile, 0, IMAGES)
                core_pass(kp, ct, pr, kh, kw)
            for m in range(M):
                core_out(ct, pr, m, nc.vector.tensor_copy)
                if index == len(late_banks) - 1:
                    store(ct, pr * M + m, 1)
            if index < len(late_banks) - 1:
                store(ct, pr * M, M)
